import numpy as np
import ml_dtypes


def mxq(x, axis, fmt="e4m3"):
    dtype, down = {"e4m3": (ml_dtypes.float8_e4m3fn, 7), "e5m2": (ml_dtypes.float8_e5m2, 14)}[fmt]
    v = np.moveaxis(np.asarray(x, np.float32).astype(ml_dtypes.bfloat16).astype(np.float64), axis, -1)
    blocks = v.reshape(v.shape[:-1] + (-1, 32))
    amax = np.abs(blocks).max(-1, keepdims=True)
    byte = np.maximum(np.where(amax > 0, np.frexp(amax)[1] - 1 + 127, 0) - down, 1)
    scale = np.exp2(byte - 127.0)
    codes = (blocks / scale).astype(np.float32).astype(dtype).astype(np.float64)
    return np.moveaxis((codes * scale).reshape(v.shape), -1, axis)


WIDE = False


def mx_kscale(k):
    if not WIDE:
        return np.ones(k)
    levels = np.array([10, -10, 5, -5, 0])
    if k % 512:
        return np.exp2(np.random.permutation(np.resize(levels, k // 32))).repeat(32)
    a = np.empty((k // 512, 16))
    for p in range(k // 512):
        a[p, :8] = np.random.permutation(np.resize(levels, 8))
        for g in range(8):
            far = levels[np.abs(levels - a[p, g]) >= 10]
            a[p, g + 8] = far[np.random.randint(len(far))]
    return np.exp2(a.ravel()).repeat(32)


BF16 = ml_dtypes.bfloat16


def bf(x):
    return np.asarray(x, np.float32).astype(BF16)


def f64(x):
    return np.asarray(x).astype(np.float64)


B, C, HH, WW, NH, HD, F = 32, 256, 16, 16, 8, 64, 1024
EPS = 1e-5


def layer_norm(v, w, b):
    mu = v.mean(-1, keepdims=True)
    var = ((v - mu) ** 2).mean(-1, keepdims=True)
    return (v - mu) * (1.0 / np.sqrt(var + EPS)) * w + b


def setup_inputs():
    s = mx_kscale(F)
    return {"h": bf(np.maximum(np.random.standard_normal((B, HH, WW, F)), 0.0) * 0.125 * s),
            "ffn2_w": bf(np.random.standard_normal((C, F)) * 0.5 / np.sqrt(F) / s),
            "ffn2_b": bf(np.random.standard_normal(C) * 0.02),
            "scale_ffn": bf(0.1 * (1.0 + 0.1 * np.random.standard_normal(1))),
            "ln2_w": bf(1.0 + 0.1 * np.random.standard_normal(C)),
            "ln2_b": bf(0.1 * np.random.standard_normal(C)),
            "scale_norm2": bf(1.5 * (1.0 + 0.1 * np.random.standard_normal(1))),
            "x": bf(np.random.standard_normal((B, C, HH, WW)))}


def reference(h, ffn2_w, ffn2_b, scale_ffn, ln2_w, ln2_b, scale_norm2, x):
    y2 = ((mxq(f64(h), 3, "e4m3") @ mxq(f64(ffn2_w), 1, "e4m3").T) + f64(ffn2_b)) * f64(scale_ffn)
    y2 = layer_norm(y2, f64(ln2_w), f64(ln2_b)) * f64(scale_norm2)
    out = np.maximum(y2 + f64(x).transpose(0, 2, 3, 1), 0.0)
    return out.transpose(0, 3, 1, 2)

@@ -1,0 +1,302 @@
+from contextlib import ExitStack
+
+import concourse.mybir as mybir
+from concourse.masks import make_identity
+
+F32 = mybir.dt.float32
+BF16 = mybir.dt.bfloat16
+U32 = mybir.dt.uint32
+U8 = mybir.dt.uint8
+FP8X4 = mybir.dt.float8_e4m3fn_x4
+ALU = mybir.AluOpType
+ACT = mybir.ActivationFunctionType
+
+P = 128
+K = 1024
+C = 256
+PIXELS = 32 * 16 * 16
+IMAGE = 16 * 16
+EPS = 1e-5
+PASSES = K // (4 * P)
+WORDS = K // 2
+BLOCKS = WORDS // P
+PARITIES = C // P
+TILES = 4
+PAIR = 2
+GROUP = TILES * P
+GROUPS = PIXELS // GROUP
+IMAGES = GROUP // IMAGE
+
+PREFETCH = 3
+
+FLOPS = 2 * PIXELS * K * C
+
+
+def transpose_words(nc, bank, words, ident):
+    for j in range(BLOCKS):
+        g, u = divmod(j, 2)
+        nc.tensor.transpose(bank[:, j, :], words[:, 2 * P * g + u : 2 * P * (g + 1) : 2], ident[:])
+
+
+def words_by_column(bank):
+    return bank[:].rearrange("p (g u) c -> p g c u", u=2)
+
+
+def tile_transformerconvblock_pc_t_kernel(
+    tc, h, ffn2_w, ffn2_b, scale_ffn, ln2_w, ln2_b, scale_norm2, x, out
+):
+    nc = tc.nc
+    h_rows = h.rearrange("b i j k -> (b i j) k")
+
+    with ExitStack() as ctx:
+        consts = ctx.enter_context(tc.tile_pool(name="consts", bufs=1))
+        h_pool = ctx.enter_context(tc.tile_pool(name="h_pool", bufs=5))
+        x_pool = ctx.enter_context(tc.tile_pool(name="x_pool", bufs=PREFETCH + 5))
+        mx_pool = ctx.enter_context(tc.tile_pool(name="mx_pool", bufs=2))
+        work = ctx.enter_context(tc.tile_pool(name="work", bufs=3))
+        stats = ctx.enter_context(tc.tile_pool(name="stats", bufs=4))
+        in_banks = ctx.enter_context(tc.psum_pool(name="in_banks", bufs=4))
+        acc_banks = ctx.enter_context(tc.psum_pool(name="acc_banks", bufs=2))
+        out_banks = ctx.enter_context(tc.psum_pool(name="out_banks", bufs=2))
+        ctx.enter_context(tc.manual_schedule())
+
+        ident = consts.tile([P, P], F32)
+        make_identity(nc, ident[:])
+        ones = consts.tile([P, P], BF16)
+        nc.vector.memset(ones[:], 1.0)
+        eps_col = consts.tile([P, 1], F32)
+        nc.vector.tensor_scalar(out=eps_col[:], in0=ones[:, 0:1], scalar1=EPS, scalar2=None, op0=ALU.mult)
+        warm = consts.tile([P, 1], F32)
+        nc.scalar.activation(out=warm[:], in_=eps_col[:], func=ACT.Sqrt)
+
+        S_AT = C
+        N_AT = C + 16
+        row = consts.tile([P, 512], BF16)
+        nc.vector.memset(row[:], 0.0)
+        nc.scalar.dma_start(out=row[0:1, 0:C], in_=ffn2_b.rearrange("(o c) -> o c", o=1))
+        nc.scalar.dma_start(out=row[0:1, S_AT : S_AT + 1], in_=scale_ffn.rearrange("(o c) -> o c", o=1))
+        nc.scalar.dma_start(out=row[0:1, N_AT : N_AT + 1], in_=scale_norm2.rearrange("(o c) -> o c", o=1))
+        ln_w = consts.tile([P, PARITIES], BF16)
+        nc.scalar.dma_start(out=ln_w[:], in_=ln2_w.rearrange("(q e) -> q e", e=PARITIES))
+        ln_b = consts.tile([P, PARITIES], BF16)
+        nc.scalar.dma_start(out=ln_b[:], in_=ln2_b.rearrange("(q e) -> q e", e=PARITIES))
+
+        w_sb = consts.tile([P, PARITIES * K], BF16)
+        nc.sync.dma_start(out=w_sb[:], in_=ffn2_w.rearrange("(q e) k -> q (e k)", e=PARITIES))
+
+        tiles = {}
+
+        def images_of(grp):
+            return slice(grp * IMAGES, (grp + 1) * IMAGES)
+
+        def load(grp):
+            h_sb = h_pool.tile([P, TILES * K], BF16, name="h_sb")
+            source = h_rows[grp * GROUP : (grp + 1) * GROUP, :].rearrange("(p t) k -> p (t k)", t=TILES)
+            pieces = TILES if grp == 0 else 1
+            width = TILES * K // pieces
+            for i in range(pieces):
+                cols = slice(i * width, (i + 1) * width)
+                nc.sync.dma_start(out=h_sb[:, cols], in_=source[:, cols])
+            x_sb = x_pool.tile([P, IMAGES, PARITIES, IMAGE], BF16, name="x_sb")
+            nc.sync.dma_start(
+                out=x_sb[:].rearrange("q b e s -> q b (e s)"),
+                in_=x[images_of(grp)].rearrange("b (q e) i j -> q b (e i j)", e=PARITIES),
+            )
+            tiles["h", grp] = h_sb
+            tiles["x", grp] = x_sb
+
+        for grp in range(PREFETCH):
+            load(grp)
+
+        w_words = w_sb[:].bitcast(F32)
+        w_grouped = consts.tile([P, PASSES * C * 4], BF16, align_bytes=64)
+        w_grouped_words = w_grouped[:].bitcast(F32).rearrange(
+            "p (g e q u) -> p g e q u", g=PASSES, e=PARITIES, u=2
+        )
+        for e in range(PARITIES):
+            w_bank = in_banks.tile([P, BLOCKS, P], F32, tag="in_bank")
+            transpose_words(nc, w_bank, w_words[:, e * WORDS : (e + 1) * WORDS], ident)
+            nc.vector.tensor_copy(out=w_grouped_words[:, :, e, :, :], in_=words_by_column(w_bank))
+        w_codes = consts.tile([P, PASSES * C], U32, align_bytes=64)
+        w_scales = consts.tile([P, PASSES * C], U8, align_bytes=64)
+        nc.vector.quantize_mx(out=w_codes[:].bitcast(FP8X4), scales=w_scales[:], in_=w_grouped[:])
+
+        row_bank = out_banks.tile([P, 512], F32, tag="out_bank")
+        nc.tensor.matmul(out=row_bank[:], lhsT=ones[:], rhs=row[:], start=True, stop=True)
+        bias_bc = consts.tile([P, C], F32)
+        nc.vector.tensor_copy(
+            out=bias_bc[:].rearrange("p (e q) -> p e q", e=PARITIES),
+            in_=row_bank[:, 0:C].rearrange("p (q e) -> p e q", e=PARITIES),
+        )
+        s_col = consts.tile([P, 1], F32)
+        nc.vector.tensor_copy(out=s_col[:], in_=row_bank[:, S_AT : S_AT + 1])
+        n_col = consts.tile([P, 1], F32)
+        nc.vector.tensor_copy(out=n_col[:], in_=row_bank[:, N_AT : N_AT + 1])
+        var_scale = consts.tile([P, 1], F32)
+        nc.vector.tensor_scalar(
+            out=var_scale[:], in0=s_col[:], scalar1=s_col[:, 0:1], scalar2=1.0 / C, op0=ALU.mult, op1=ALU.mult
+        )
+        gain = consts.tile([P, PARITIES], F32)
+        nc.vector.tensor_scalar(
+            out=gain[:], in0=ln_w[:], scalar1=n_col[:, 0:1], scalar2=s_col[:, 0:1], op0=ALU.mult, op1=ALU.mult
+        )
+        shift = consts.tile([P, PARITIES], F32)
+        nc.vector.tensor_scalar(out=shift[:], in0=ln_b[:], scalar1=n_col[:, 0:1], scalar2=None, op0=ALU.mult)
+
+        def transpose_in(grp, half):
+            if half == 0:
+                tiles["grouped", grp] = mx_pool.tile([P, TILES * K], BF16, name="h_grouped", align_bytes=64)
+            h_words = tiles["h", grp][:].bitcast(F32)
+            h_grouped_words = tiles["grouped", grp][:].bitcast(F32).rearrange(
+                "p (t g c u) -> p t g c u", t=TILES, g=PASSES, u=2
+            )
+            for t in range(half * PAIR, (half + 1) * PAIR):
+                h_bank = in_banks.tile([P, BLOCKS, P], F32, tag="in_bank")
+                transpose_words(nc, h_bank, h_words[:, t * WORDS : (t + 1) * WORDS], ident)
+                nc.scalar.copy(out=h_grouped_words[:, t, :, :, :], in_=words_by_column(h_bank))
+
+        def quantise(grp, half):
+            if half == 0:
+                tiles["codes", grp] = mx_pool.tile([P, TILES * PASSES * P], U32, name="h_codes", align_bytes=64)
+                tiles["scales", grp] = mx_pool.tile([P, TILES * PASSES * P], U8, name="h_scales", align_bytes=64)
+            words = slice(half * PAIR * PASSES * P, (half + 1) * PAIR * PASSES * P)
+            values = slice(half * PAIR * K, (half + 1) * PAIR * K)
+            nc.vector.quantize_mx(
+                out=tiles["codes", grp][:, words].bitcast(FP8X4),
+                scales=tiles["scales", grp][:, words],
+                in_=tiles["grouped", grp][:, values],
+            )
+
+        def multiply(grp, half):
+            if half == 0:
+                tiles["v", grp] = work.tile([P, TILES, C], F32, name="v")
+                tiles["v_sum", grp] = stats.tile([P, TILES], F32, name="v_sum")
+            h_codes = tiles["codes", grp]
+            h_scales = tiles["scales", grp]
+            acc = acc_banks.tile([P, PAIR, C], F32)
+            for i in range(PAIR):
+                for g in range(PASSES):
+                    px = slice(((half * PAIR + i) * PASSES + g) * P, ((half * PAIR + i) * PASSES + g + 1) * P)
+                    ch = slice(g * C, (g + 1) * C)
+                    nc.tensor.matmul_mx(
+                        out=acc[:, i, :],
+                        lhsT=h_codes[:, px].bitcast(FP8X4),
+                        lhsT_scale=h_scales[:, px],
+                        rhs=w_codes[:, ch].bitcast(FP8X4),
+                        rhs_scale=w_scales[:, ch],
+                        start=(g == 0),
+                        stop=(g == PASSES - 1),
+                    )
+            for i in range(PAIR):
+                t = half * PAIR + i
+                nc.vector.scalar_tensor_tensor(
+                    out=tiles["v", grp][:, t, :],
+                    in0=acc[:, i, :],
+                    scalar=1.0,
+                    in1=bias_bc[:],
+                    op0=ALU.mult,
+                    op1=ALU.add,
+                    accum_out=tiles["v_sum", grp][:, t : t + 1],
+                )
+
+        def mean(grp):
+            neg_mean = stats.tile([P, TILES], F32, name="neg_mean")
+            nc.vector.tensor_scalar(
+                out=neg_mean[:], in0=tiles["v_sum", grp][:], scalar1=-1.0 / C, scalar2=None, op0=ALU.mult
+            )
+            tiles["neg_mean", grp] = neg_mean
+
+        def squares(grp):
+            v = tiles["v", grp]
+            neg_mean = tiles["neg_mean", grp]
+            squared = work.tile([P, TILES, C], F32, name="squared")
+            sq_sum = stats.tile([P, TILES], F32, name="sq_sum")
+            for t in range(TILES):
+                nc.scalar.activation(
+                    out=squared[:, t, :],
+                    in_=v[:, t, :],
+                    func=ACT.Square,
+                    bias=neg_mean[:, t : t + 1],
+                    scale=1.0,
+                    accum_out=sq_sum[:, t : t + 1],
+                )
+            std = stats.tile([P, TILES], F32, name="std")
+            nc.scalar.activation(
+                out=std[:], in_=sq_sum[:], func=ACT.Sqrt, bias=eps_col[:, 0:1], scale=var_scale[:, 0:1]
+            )
+            tiles["std", grp] = std
+
+        def normalise(grp):
+            v = tiles["v", grp]
+            neg_mean = tiles["neg_mean", grp]
+            rstd = stats.tile([P, TILES], F32, name="rstd")
+            nc.vector.reciprocal(out=rstd[:], in_=tiles["std", grp][:])
+            normed = work.tile([P, TILES, C], F32, name="normed")
+            for t in range(TILES):
+                nc.vector.tensor_scalar(
+                    out=normed[:, t, :],
+                    in0=v[:, t, :],
+                    scalar1=neg_mean[:, t : t + 1],
+                    scalar2=rstd[:, t : t + 1],
+                    op0=ALU.add,
+                    op1=ALU.mult,
+                )
+            tiles["normed", grp] = normed
+
+        def transpose_out(grp, e):
+            if e == 0:
+                tiles["o", grp] = work.tile([P, IMAGES, PARITIES, IMAGE], F32, name="o_sb")
+            o_bank = out_banks.tile([P, TILES, P], F32, tag="out_bank")
+            for t in range(TILES):
+                nc.tensor.transpose(o_bank[:, t, :], tiles["normed", grp][:, t, e * P : (e + 1) * P], ident[:])
+            nc.vector.scalar_tensor_tensor(
+                out=tiles["o", grp][:, :, e, :].rearrange("q b (p t) -> q b p t", t=TILES),
+                in0=o_bank[:].rearrange("q t (b p) -> q b p t", b=IMAGES),
+                scalar=gain[:, e : e + 1],
+                in1=tiles["x", grp][:, :, e, :].rearrange("q b (p t) -> q b p t", t=TILES),
+                op0=ALU.mult,
+                op1=ALU.add,
+            )
+
+        def relu_store(grp):
+            o_sb = tiles["o", grp]
+            for e in range(PARITIES):
+                nc.scalar.activation(
+                    out=o_sb[:, :, e, :], in_=o_sb[:, :, e, :], func=ACT.Relu, bias=shift[:, e : e + 1], scale=1.0
+                )
+            nc.sync.dma_start(
+                out=out[images_of(grp)].rearrange("b (q e) i j -> q b (e i j)", e=PARITIES),
+                in_=o_sb[:].rearrange("q b e s -> q b (e s)"),
+            )
+
+        def is_group(grp):
+            return 0 <= grp < GROUPS
+
+        for step in range(GROUPS + 4):
+            if is_group(step + PREFETCH):
+                load(step + PREFETCH)
+
+            if is_group(step):
+                transpose_in(step, 0)
+            if is_group(step - 1):
+                multiply(step - 1, 0)
+            if is_group(step - 4):
+                transpose_out(step - 4, 1)
+            if is_group(step):
+                quantise(step, 0)
+            if is_group(step - 2):
+                squares(step - 2)
+
+            if is_group(step):
+                transpose_in(step, 1)
+            if is_group(step - 1):
+                multiply(step - 1, 1)
+                mean(step - 1)
+            if is_group(step - 3):
+                transpose_out(step - 3, 0)
+            if is_group(step - 2):
+                normalise(step - 2)
+            if is_group(step):
+                quantise(step, 1)
+            if is_group(step - 4):
+                relu_store(step - 4)

@@ -14,19 +14,16 @@ ACT = mybir.ActivationFunctionType
 P = 128
 K = 1024
 C = 256
-PIXELS = 32 * 16 * 16
+IMAGES = 32
 IMAGE = 16 * 16
+PIXELS = IMAGES * IMAGE
 EPS = 1e-5
 PASSES = K // (4 * P)
 WORDS = K // 2
 BLOCKS = WORDS // P
 PARITIES = C // P
-TILES = 4
-PAIR = 2
-GROUP = TILES * P
-GROUPS = PIXELS // GROUP
-IMAGES = GROUP // IMAGE
-
+TILES = IMAGE // P
+LOAD = 2
 PREFETCH = 3
 
 FLOPS = 2 * PIXELS * K * C
@@ -52,7 +49,7 @@ def tile_transformerconvblock_pc_t_kernel(
         consts = ctx.enter_context(tc.tile_pool(name="consts", bufs=1))
         h_pool = ctx.enter_context(tc.tile_pool(name="h_pool", bufs=5))
         x_pool = ctx.enter_context(tc.tile_pool(name="x_pool", bufs=PREFETCH + 5))
-        mx_pool = ctx.enter_context(tc.tile_pool(name="mx_pool", bufs=2))
+        mx_pool = ctx.enter_context(tc.tile_pool(name="mx_pool", bufs=3))
         work = ctx.enter_context(tc.tile_pool(name="work", bufs=3))
         stats = ctx.enter_context(tc.tile_pool(name="stats", bufs=4))
         in_banks = ctx.enter_context(tc.psum_pool(name="in_banks", bufs=4))
@@ -67,7 +64,7 @@ def tile_transformerconvblock_pc_t_kernel(
         eps_col = consts.tile([P, 1], F32)
         nc.vector.tensor_scalar(out=eps_col[:], in0=ones[:, 0:1], scalar1=EPS, scalar2=None, op0=ALU.mult)
         warm = consts.tile([P, 1], F32)
-        nc.scalar.activation(out=warm[:], in_=eps_col[:], func=ACT.Sqrt)
+        nc.scalar.activation(out=warm[:], in_=eps_col[:], func=ACT.Abs_reciprocal_sqrt)
 
         S_AT = C
         N_AT = C + 16
@@ -86,27 +83,29 @@ def tile_transformerconvblock_pc_t_kernel(
 
         tiles = {}
 
-        def images_of(grp):
-            return slice(grp * IMAGES, (grp + 1) * IMAGES)
-
-        def load(grp):
-            h_sb = h_pool.tile([P, TILES * K], BF16, name="h_sb")
-            source = h_rows[grp * GROUP : (grp + 1) * GROUP, :].rearrange("(p t) k -> p (t k)", t=TILES)
-            pieces = TILES if grp == 0 else 1
-            width = TILES * K // pieces
-            for i in range(pieces):
-                cols = slice(i * width, (i + 1) * width)
-                nc.sync.dma_start(out=h_sb[:, cols], in_=source[:, cols])
-            x_sb = x_pool.tile([P, IMAGES, PARITIES, IMAGE], BF16, name="x_sb")
+        def load(n):
+            h_sb = h_pool.tile([P, LOAD, TILES * K], BF16, name="h_sb")
+            source = h_rows[n * LOAD * IMAGE : (n + 1) * LOAD * IMAGE, :].rearrange(
+                "(b p t) k -> p b (t k)", b=LOAD, t=TILES
+            )
+            if n == 0:
+                for b in range(LOAD):
+                    for t in range(TILES):
+                        nc.sync.dma_start(
+                            out=h_sb[:, b, t * K : (t + 1) * K], in_=source[:, b, t * K : (t + 1) * K]
+                        )
+            else:
+                nc.sync.dma_start(out=h_sb[:], in_=source)
+            tiles["h", n] = h_sb
+            x_sb = x_pool.tile([P, LOAD, PARITIES, IMAGE], BF16, name="x_sb")
             nc.sync.dma_start(
                 out=x_sb[:].rearrange("q b e s -> q b (e s)"),
-                in_=x[images_of(grp)].rearrange("b (q e) i j -> q b (e i j)", e=PARITIES),
+                in_=x[n * LOAD : (n + 1) * LOAD].rearrange("b (q e) i j -> q b (e i j)", e=PARITIES),
             )
-            tiles["h", grp] = h_sb
-            tiles["x", grp] = x_sb
+            tiles["x", n] = x_sb
 
-        for grp in range(PREFETCH):
-            load(grp)
+        for n in range(PREFETCH):
+            load(n)
 
         w_words = w_sb[:].bitcast(F32)
         w_grouped = consts.tile([P, PASSES * C * 4], BF16, align_bytes=64)
@@ -134,7 +133,7 @@ def tile_transformerconvblock_pc_t_kernel(
         nc.vector.tensor_copy(out=n_col[:], in_=row_bank[:, N_AT : N_AT + 1])
         var_scale = consts.tile([P, 1], F32)
         nc.vector.tensor_scalar(
-            out=var_scale[:], in0=s_col[:], scalar1=s_col[:, 0:1], scalar2=1.0 / C, op0=ALU.mult, op1=ALU.mult
+            out=var_scale[:], in0=s_col[:], scalar1=s_col[:, 0:1], scalar2=1.0 / C**3, op0=ALU.mult, op1=ALU.mult
         )
         gain = consts.tile([P, PARITIES], F32)
         nc.vector.tensor_scalar(
@@ -143,72 +142,68 @@ def tile_transformerconvblock_pc_t_kernel(
         shift = consts.tile([P, PARITIES], F32)
         nc.vector.tensor_scalar(out=shift[:], in0=ln_b[:], scalar1=n_col[:, 0:1], scalar2=None, op0=ALU.mult)
 
-        def transpose_in(grp, half):
-            if half == 0:
-                tiles["grouped", grp] = mx_pool.tile([P, TILES * K], BF16, name="h_grouped", align_bytes=64)
-            h_words = tiles["h", grp][:].bitcast(F32)
-            h_grouped_words = tiles["grouped", grp][:].bitcast(F32).rearrange(
-                "p (t g c u) -> p t g c u", t=TILES, g=PASSES, u=2
-            )
-            for t in range(half * PAIR, (half + 1) * PAIR):
+        def transpose_in(i):
+            n, b = divmod(i, LOAD)
+            grouped = mx_pool.tile([P, TILES * K], BF16, name="h_grouped", align_bytes=64)
+            h_words = tiles["h", n][:, b, :].bitcast(F32)
+            grouped_words = grouped[:].bitcast(F32).rearrange("p (t g c u) -> p t g c u", t=TILES, g=PASSES, u=2)
+            for t in range(TILES):
                 h_bank = in_banks.tile([P, BLOCKS, P], F32, tag="in_bank")
                 transpose_words(nc, h_bank, h_words[:, t * WORDS : (t + 1) * WORDS], ident)
-                nc.scalar.copy(out=h_grouped_words[:, t, :, :, :], in_=words_by_column(h_bank))
+                nc.scalar.copy(out=grouped_words[:, t, :, :, :], in_=words_by_column(h_bank))
+            tiles["grouped", i] = grouped
 
-        def quantise(grp, half):
-            if half == 0:
-                tiles["codes", grp] = mx_pool.tile([P, TILES * PASSES * P], U32, name="h_codes", align_bytes=64)
-                tiles["scales", grp] = mx_pool.tile([P, TILES * PASSES * P], U8, name="h_scales", align_bytes=64)
-            words = slice(half * PAIR * PASSES * P, (half + 1) * PAIR * PASSES * P)
-            values = slice(half * PAIR * K, (half + 1) * PAIR * K)
-            nc.vector.quantize_mx(
-                out=tiles["codes", grp][:, words].bitcast(FP8X4),
-                scales=tiles["scales", grp][:, words],
-                in_=tiles["grouped", grp][:, values],
-            )
+        def quantise(i):
+            codes = mx_pool.tile([P, TILES * PASSES * P], U32, name="h_codes", align_bytes=64)
+            scales = mx_pool.tile([P, TILES * PASSES * P], U8, name="h_scales", align_bytes=64)
+            nc.vector.quantize_mx(out=codes[:].bitcast(FP8X4), scales=scales[:], in_=tiles["grouped", i][:])
+            tiles["mx", i] = codes, scales
 
-        def multiply(grp, half):
-            if half == 0:
-                tiles["v", grp] = work.tile([P, TILES, C], F32, name="v")
-                tiles["v_sum", grp] = stats.tile([P, TILES], F32, name="v_sum")
-            h_codes = tiles["codes", grp]
-            h_scales = tiles["scales", grp]
-            acc = acc_banks.tile([P, PAIR, C], F32)
-            for i in range(PAIR):
+        def multiply(i):
+            codes, scales = tiles["mx", i]
+            acc = acc_banks.tile([P, TILES, C], F32, name="acc")
+            for t in range(TILES):
                 for g in range(PASSES):
-                    px = slice(((half * PAIR + i) * PASSES + g) * P, ((half * PAIR + i) * PASSES + g + 1) * P)
+                    px = slice((t * PASSES + g) * P, (t * PASSES + g + 1) * P)
                     ch = slice(g * C, (g + 1) * C)
                     nc.tensor.matmul_mx(
-                        out=acc[:, i, :],
-                        lhsT=h_codes[:, px].bitcast(FP8X4),
-                        lhsT_scale=h_scales[:, px],
+                        out=acc[:, t, :],
+                        lhsT=codes[:, px].bitcast(FP8X4),
+                        lhsT_scale=scales[:, px],
                         rhs=w_codes[:, ch].bitcast(FP8X4),
                         rhs_scale=w_scales[:, ch],
                         start=(g == 0),
                         stop=(g == PASSES - 1),
                     )
-            for i in range(PAIR):
-                t = half * PAIR + i
+            tiles["acc", i] = acc
+
+        def add_bias(i):
+            acc = tiles["acc", i]
+            v = work.tile([P, TILES, C], F32, name="v")
+            v_sum = stats.tile([P, TILES], F32, name="v_sum")
+            for t in range(TILES):
                 nc.vector.scalar_tensor_tensor(
-                    out=tiles["v", grp][:, t, :],
-                    in0=acc[:, i, :],
+                    out=v[:, t, :],
+                    in0=acc[:, t, :],
                     scalar=1.0,
                     in1=bias_bc[:],
                     op0=ALU.mult,
                     op1=ALU.add,
-                    accum_out=tiles["v_sum", grp][:, t : t + 1],
+                    accum_out=v_sum[:, t : t + 1],
                 )
+            tiles["v", i] = v
+            tiles["v_sum", i] = v_sum
 
-        def mean(grp):
+        def mean(i):
             neg_mean = stats.tile([P, TILES], F32, name="neg_mean")
             nc.vector.tensor_scalar(
-                out=neg_mean[:], in0=tiles["v_sum", grp][:], scalar1=-1.0 / C, scalar2=None, op0=ALU.mult
+                out=neg_mean[:], in0=tiles["v_sum", i][:], scalar1=-1.0 / C, scalar2=None, op0=ALU.mult
             )
-            tiles["neg_mean", grp] = neg_mean
+            tiles["neg_mean", i] = neg_mean
 
-        def squares(grp):
-            v = tiles["v", grp]
-            neg_mean = tiles["neg_mean", grp]
+        def squares(i):
+            v = tiles["v", i]
+            v_sum = tiles["v_sum", i]
             squared = work.tile([P, TILES, C], F32, name="squared")
             sq_sum = stats.tile([P, TILES], F32, name="sq_sum")
             for t in range(TILES):
@@ -216,21 +211,27 @@ def tile_transformerconvblock_pc_t_kernel(
                     out=squared[:, t, :],
                     in_=v[:, t, :],
                     func=ACT.Square,
-                    bias=neg_mean[:, t : t + 1],
-                    scale=1.0,
+                    bias=v_sum[:, t : t + 1],
+                    scale=-float(C),
                     accum_out=sq_sum[:, t : t + 1],
                 )
-            std = stats.tile([P, TILES], F32, name="std")
-            nc.scalar.activation(
-                out=std[:], in_=sq_sum[:], func=ACT.Sqrt, bias=eps_col[:, 0:1], scale=var_scale[:, 0:1]
-            )
-            tiles["std", grp] = std
+            tiles["sq_sum", i] = sq_sum
 
-        def normalise(grp):
-            v = tiles["v", grp]
-            neg_mean = tiles["neg_mean", grp]
+        def inverse_std(i):
             rstd = stats.tile([P, TILES], F32, name="rstd")
-            nc.vector.reciprocal(out=rstd[:], in_=tiles["std", grp][:])
+            nc.scalar.activation(
+                out=rstd[:],
+                in_=tiles["sq_sum", i][:],
+                func=ACT.Abs_reciprocal_sqrt,
+                bias=eps_col[:, 0:1],
+                scale=var_scale[:, 0:1],
+            )
+            tiles["rstd", i] = rstd
+
+        def normalise(i):
+            v = tiles["v", i]
+            neg_mean = tiles["neg_mean", i]
+            rstd = tiles["rstd", i]
             normed = work.tile([P, TILES, C], F32, name="normed")
             for t in range(TILES):
                 nc.vector.tensor_scalar(
@@ -241,62 +242,65 @@ def tile_transformerconvblock_pc_t_kernel(
                     op0=ALU.add,
                     op1=ALU.mult,
                 )
-            tiles["normed", grp] = normed
+            tiles["normed", i] = normed
 
-        def transpose_out(grp, e):
-            if e == 0:
-                tiles["o", grp] = work.tile([P, IMAGES, PARITIES, IMAGE], F32, name="o_sb")
-            o_bank = out_banks.tile([P, TILES, P], F32, tag="out_bank")
-            for t in range(TILES):
-                nc.tensor.transpose(o_bank[:, t, :], tiles["normed", grp][:, t, e * P : (e + 1) * P], ident[:])
-            nc.vector.scalar_tensor_tensor(
-                out=tiles["o", grp][:, :, e, :].rearrange("q b (p t) -> q b p t", t=TILES),
-                in0=o_bank[:].rearrange("q t (b p) -> q b p t", b=IMAGES),
-                scalar=gain[:, e : e + 1],
-                in1=tiles["x", grp][:, :, e, :].rearrange("q b (p t) -> q b p t", t=TILES),
-                op0=ALU.mult,
-                op1=ALU.add,
-            )
+        def transpose_out(i):
+            o_bank = out_banks.tile([P, PARITIES, TILES, P], F32, tag="out_bank")
+            for e in range(PARITIES):
+                for t in range(TILES):
+                    nc.tensor.transpose(o_bank[:, e, t, :], tiles["normed", i][:, t, e * P : (e + 1) * P], ident[:])
+            tiles["o_bank", i] = o_bank
 
-        def relu_store(grp):
-            o_sb = tiles["o", grp]
+        def add_x(i):
+            n, b = divmod(i, LOAD)
+            o_sb = work.tile([P, PARITIES, IMAGE], F32, name="o_sb", bufs=6)
+            for e in range(PARITIES):
+                nc.vector.scalar_tensor_tensor(
+                    out=o_sb[:, e, :].rearrange("q (p t) -> q p t", t=TILES),
+                    in0=tiles["o_bank", i][:, e, :, :].rearrange("q t p -> q p t"),
+                    scalar=gain[:, e : e + 1],
+                    in1=tiles["x", n][:, b, e, :].rearrange("q (p t) -> q p t", t=TILES),
+                    op0=ALU.mult,
+                    op1=ALU.add,
+                )
+            tiles["o", i] = o_sb
+
+        def relu_store(i):
+            o_sb = tiles["o", i]
             for e in range(PARITIES):
                 nc.scalar.activation(
-                    out=o_sb[:, :, e, :], in_=o_sb[:, :, e, :], func=ACT.Relu, bias=shift[:, e : e + 1], scale=1.0
+                    out=o_sb[:, e, :], in_=o_sb[:, e, :], func=ACT.Relu, bias=shift[:, e : e + 1], scale=1.0
                 )
             nc.sync.dma_start(
-                out=out[images_of(grp)].rearrange("b (q e) i j -> q b (e i j)", e=PARITIES),
-                in_=o_sb[:].rearrange("q b e s -> q b (e s)"),
+                out=out[i].rearrange("(q e) i j -> q (e i j)", e=PARITIES),
+                in_=o_sb[:].rearrange("q e s -> q (e s)"),
             )
 
-        def is_group(grp):
-            return 0 <= grp < GROUPS
+        def is_image(i):
+            return 0 <= i < IMAGES
 
-        for step in range(GROUPS + 4):
-            if is_group(step + PREFETCH):
-                load(step + PREFETCH)
-
-            if is_group(step):
-                transpose_in(step, 0)
-            if is_group(step - 1):
-                multiply(step - 1, 0)
-            if is_group(step - 4):
-                transpose_out(step - 4, 1)
-            if is_group(step):
-                quantise(step, 0)
-            if is_group(step - 2):
+        for step in range(IMAGES + 6):
+            if step % LOAD == 0 and step // LOAD + PREFETCH < IMAGES // LOAD:
+                load(step // LOAD + PREFETCH)
+            if is_image(step):
+                transpose_in(step)
+            if is_image(step - 4):
+                transpose_out(step - 4)
+            if is_image(step - 1):
+                quantise(step - 1)
+            if is_image(step - 1):
+                multiply(step - 1)
+            if is_image(step - 2):
+                add_bias(step - 2)
+            if is_image(step - 4):
+                add_x(step - 4)
+            if is_image(step - 2):
+                mean(step - 2)
+            if is_image(step - 2):
                 squares(step - 2)
-
-            if is_group(step):
-                transpose_in(step, 1)
-            if is_group(step - 1):
-                multiply(step - 1, 1)
-                mean(step - 1)
-            if is_group(step - 3):
-                transpose_out(step - 3, 0)
-            if is_group(step - 2):
-                normalise(step - 2)
-            if is_group(step):
-                quantise(step, 1)
-            if is_group(step - 4):
-                relu_store(step - 4)
+            if is_image(step - 2):
+                inverse_std(step - 2)
+            if is_image(step - 3):
+                normalise(step - 3)
+            if is_image(step - 5):
+                relu_store(step - 5)

@@ -23,6 +23,7 @@ WORDS = K // 2
 BLOCKS = WORDS // P
 PARITIES = C // P
 TILES = IMAGE // P
+SPLIT = 1
 LOAD = 2
 PREFETCH = 3
 
@@ -50,8 +51,8 @@ def tile_transformerconvblock_pc_t_kernel(
         h_pool = ctx.enter_context(tc.tile_pool(name="h_pool", bufs=5))
         x_pool = ctx.enter_context(tc.tile_pool(name="x_pool", bufs=PREFETCH + 5))
         mx_pool = ctx.enter_context(tc.tile_pool(name="mx_pool", bufs=3))
-        work = ctx.enter_context(tc.tile_pool(name="work", bufs=3))
-        stats = ctx.enter_context(tc.tile_pool(name="stats", bufs=4))
+        work = ctx.enter_context(tc.tile_pool(name="work", bufs=4))
+        stats = ctx.enter_context(tc.tile_pool(name="stats", bufs=6))
         in_banks = ctx.enter_context(tc.psum_pool(name="in_banks", bufs=4))
         acc_banks = ctx.enter_context(tc.psum_pool(name="acc_banks", bufs=2))
         out_banks = ctx.enter_context(tc.psum_pool(name="out_banks", bufs=2))
@@ -196,7 +197,7 @@ def tile_transformerconvblock_pc_t_kernel(
 
         def mean(i):
             neg_mean = stats.tile([P, TILES], F32, name="neg_mean")
-            nc.vector.tensor_scalar(
+            nc.gpsimd.tensor_scalar(
                 out=neg_mean[:], in0=tiles["v_sum", i][:], scalar1=-1.0 / C, scalar2=None, op0=ALU.mult
             )
             tiles["neg_mean", i] = neg_mean
@@ -228,21 +229,34 @@ def tile_transformerconvblock_pc_t_kernel(
             )
             tiles["rstd", i] = rstd
 
-        def normalise(i):
-            v = tiles["v", i]
-            neg_mean = tiles["neg_mean", i]
-            rstd = tiles["rstd", i]
-            normed = work.tile([P, TILES, C], F32, name="normed")
-            for t in range(TILES):
+        def offsets(i):
+            offset = stats.tile([P, TILES], F32, name="offset")
+            nc.gpsimd.tensor_tensor(
+                out=offset[:], in0=tiles["neg_mean", i][:], in1=tiles["rstd", i][:], op=ALU.mult
+            )
+            tiles["offset", i] = offset
+            tiles["normed", i] = work.tile([P, TILES, C], F32, name="normed")
+
+        def normalise_on_vector(i):
+            for t in range(SPLIT):
                 nc.vector.tensor_scalar(
-                    out=normed[:, t, :],
-                    in0=v[:, t, :],
-                    scalar1=neg_mean[:, t : t + 1],
-                    scalar2=rstd[:, t : t + 1],
+                    out=tiles["normed", i][:, t, :],
+                    in0=tiles["v", i][:, t, :],
+                    scalar1=tiles["neg_mean", i][:, t : t + 1],
+                    scalar2=tiles["rstd", i][:, t : t + 1],
                     op0=ALU.add,
                     op1=ALU.mult,
                 )
-            tiles["normed", i] = normed
+
+        def normalise_on_scalar(i):
+            for t in range(SPLIT, TILES):
+                nc.scalar.activation(
+                    out=tiles["normed", i][:, t, :],
+                    in_=tiles["v", i][:, t, :],
+                    func=ACT.Identity,
+                    bias=tiles["offset", i][:, t : t + 1],
+                    scale=tiles["rstd", i][:, t : t + 1],
+                )
 
         def transpose_out(i):
             o_bank = out_banks.tile([P, PARITIES, TILES, P], F32, tag="out_bank")
@@ -268,8 +282,13 @@ def tile_transformerconvblock_pc_t_kernel(
         def relu_store(i):
             o_sb = tiles["o", i]
             for e in range(PARITIES):
-                nc.scalar.activation(
-                    out=o_sb[:, e, :], in_=o_sb[:, e, :], func=ACT.Relu, bias=shift[:, e : e + 1], scale=1.0
+                nc.gpsimd.tensor_scalar(
+                    out=o_sb[:, e, :],
+                    in0=o_sb[:, e, :],
+                    scalar1=shift[:, e : e + 1],
+                    scalar2=0.0,
+                    op0=ALU.add,
+                    op1=ALU.max,
                 )
             nc.sync.dma_start(
                 out=out[i].rearrange("(q e) i j -> q (e i j)", e=PARITIES),
@@ -279,28 +298,32 @@ def tile_transformerconvblock_pc_t_kernel(
         def is_image(i):
             return 0 <= i < IMAGES
 
-        for step in range(IMAGES + 6):
+        for step in range(IMAGES + 7):
             if step % LOAD == 0 and step // LOAD + PREFETCH < IMAGES // LOAD:
                 load(step // LOAD + PREFETCH)
             if is_image(step):
                 transpose_in(step)
-            if is_image(step - 4):
-                transpose_out(step - 4)
-            if is_image(step - 1):
-                quantise(step - 1)
-            if is_image(step - 1):
-                multiply(step - 1)
-            if is_image(step - 2):
-                add_bias(step - 2)
-            if is_image(step - 4):
-                add_x(step - 4)
             if is_image(step - 2):
                 mean(step - 2)
-            if is_image(step - 2):
-                squares(step - 2)
-            if is_image(step - 2):
-                inverse_std(step - 2)
             if is_image(step - 3):
-                normalise(step - 3)
+                squares(step - 3)
+            if is_image(step - 5):
+                transpose_out(step - 5)
+            if is_image(step - 5):
+                add_x(step - 5)
+            if is_image(step):
+                quantise(step)
+            if is_image(step - 4):
+                normalise_on_scalar(step - 4)
+            if is_image(step - 3):
+                inverse_std(step - 3)
+            if is_image(step - 3):
+                offsets(step - 3)
+            if is_image(step - 1):
+                multiply(step - 1)
+            if is_image(step - 1):
+                add_bias(step - 1)
+            if is_image(step - 3):
+                normalise_on_vector(step - 3)
             if is_image(step - 5):
                 relu_store(step - 5)

@@ -235,28 +235,19 @@ def tile_transformerconvblock_pc_t_kernel(
                 out=offset[:], in0=tiles["neg_mean", i][:], in1=tiles["rstd", i][:], op=ALU.mult
             )
             tiles["offset", i] = offset
-            tiles["normed", i] = work.tile([P, TILES, C], F32, name="normed")
 
-        def normalise_on_vector(i):
-            for t in range(SPLIT):
-                nc.vector.tensor_scalar(
-                    out=tiles["normed", i][:, t, :],
+        def normalise(i):
+            normed = work.tile([P, TILES, C], F32, name="normed")
+            for t in range(TILES):
+                nc.gpsimd.tensor_scalar(
+                    out=normed[:, t, :],
                     in0=tiles["v", i][:, t, :],
-                    scalar1=tiles["neg_mean", i][:, t : t + 1],
-                    scalar2=tiles["rstd", i][:, t : t + 1],
-                    op0=ALU.add,
-                    op1=ALU.mult,
+                    scalar1=tiles["rstd", i][:, t : t + 1],
+                    scalar2=tiles["offset", i][:, t : t + 1],
+                    op0=ALU.mult,
+                    op1=ALU.add,
                 )
-
-        def normalise_on_scalar(i):
-            for t in range(SPLIT, TILES):
-                nc.scalar.activation(
-                    out=tiles["normed", i][:, t, :],
-                    in_=tiles["v", i][:, t, :],
-                    func=ACT.Identity,
-                    bias=tiles["offset", i][:, t : t + 1],
-                    scale=tiles["rstd", i][:, t : t + 1],
-                )
+            tiles["normed", i] = normed
 
         def transpose_out(i):
             o_bank = out_banks.tile([P, PARITIES, TILES, P], F32, tag="out_bank")
@@ -279,20 +270,31 @@ def tile_transformerconvblock_pc_t_kernel(
                 )
             tiles["o", i] = o_sb
 
-        def relu_store(i):
-            o_sb = tiles["o", i]
-            for e in range(PARITIES):
-                nc.gpsimd.tensor_scalar(
-                    out=o_sb[:, e, :],
-                    in0=o_sb[:, e, :],
+        def relu_on_vector(i):
+            for e in range(SPLIT):
+                nc.vector.tensor_scalar(
+                    out=tiles["o", i][:, e, :],
+                    in0=tiles["o", i][:, e, :],
                     scalar1=shift[:, e : e + 1],
                     scalar2=0.0,
                     op0=ALU.add,
                     op1=ALU.max,
                 )
+
+        def relu_on_scalar(i):
+            for e in range(SPLIT, PARITIES):
+                nc.scalar.activation(
+                    out=tiles["o", i][:, e, :],
+                    in_=tiles["o", i][:, e, :],
+                    func=ACT.Relu,
+                    bias=shift[:, e : e + 1],
+                    scale=1.0,
+                )
+
+        def store(i):
             nc.sync.dma_start(
                 out=out[i].rearrange("(q e) i j -> q (e i j)", e=PARITIES),
-                in_=o_sb[:].rearrange("q e s -> q (e s)"),
+                in_=tiles["o", i][:].rearrange("q e s -> q (e s)"),
             )
 
         def is_image(i):
@@ -304,26 +306,28 @@ def tile_transformerconvblock_pc_t_kernel(
             if is_image(step):
                 transpose_in(step)
             if is_image(step - 2):
-                mean(step - 2)
-            if is_image(step - 3):
-                squares(step - 3)
+                squares(step - 2)
             if is_image(step - 5):
                 transpose_out(step - 5)
+            if is_image(step - 6):
+                relu_on_scalar(step - 6)
             if is_image(step - 5):
                 add_x(step - 5)
-            if is_image(step):
-                quantise(step)
-            if is_image(step - 4):
-                normalise_on_scalar(step - 4)
             if is_image(step - 3):
-                inverse_std(step - 3)
+                mean(step - 3)
+            if is_image(step - 2):
+                inverse_std(step - 2)
+            if is_image(step - 5):
+                relu_on_vector(step - 5)
             if is_image(step - 3):
                 offsets(step - 3)
+            if is_image(step):
+                quantise(step)
+            if is_image(step - 3):
+                normalise(step - 3)
             if is_image(step - 1):
                 multiply(step - 1)
+            if is_image(step - 6):
+                store(step - 6)
             if is_image(step - 1):
                 add_bias(step - 1)
-            if is_image(step - 3):
-                normalise_on_vector(step - 3)
-            if is_image(step - 5):
-                relu_store(step - 5)

@@ -23,9 +23,11 @@ WORDS = K // 2
 BLOCKS = WORDS // P
 PARITIES = C // P
 TILES = IMAGE // P
-SPLIT = 1
+ON_VECTOR = 0
 LOAD = 2
-PREFETCH = 3
+LOADS = IMAGES // LOAD
+PREFETCH = 4
+X_PREFETCH = 1
 
 FLOPS = 2 * PIXELS * K * C
 
@@ -48,11 +50,11 @@ def tile_transformerconvblock_pc_t_kernel(
 
     with ExitStack() as ctx:
         consts = ctx.enter_context(tc.tile_pool(name="consts", bufs=1))
-        h_pool = ctx.enter_context(tc.tile_pool(name="h_pool", bufs=5))
-        x_pool = ctx.enter_context(tc.tile_pool(name="x_pool", bufs=PREFETCH + 5))
+        h_pool = ctx.enter_context(tc.tile_pool(name="h_pool", bufs=6))
+        x_pool = ctx.enter_context(tc.tile_pool(name="x_pool", bufs=PREFETCH + 6))
         mx_pool = ctx.enter_context(tc.tile_pool(name="mx_pool", bufs=3))
-        work = ctx.enter_context(tc.tile_pool(name="work", bufs=4))
-        stats = ctx.enter_context(tc.tile_pool(name="stats", bufs=6))
+        work = ctx.enter_context(tc.tile_pool(name="work", bufs=6))
+        stats = ctx.enter_context(tc.tile_pool(name="stats", bufs=5))
         in_banks = ctx.enter_context(tc.psum_pool(name="in_banks", bufs=4))
         acc_banks = ctx.enter_context(tc.psum_pool(name="acc_banks", bufs=2))
         out_banks = ctx.enter_context(tc.psum_pool(name="out_banks", bufs=2))
@@ -79,25 +81,18 @@ def tile_transformerconvblock_pc_t_kernel(
         ln_b = consts.tile([P, PARITIES], BF16)
         nc.scalar.dma_start(out=ln_b[:], in_=ln2_b.rearrange("(q e) -> q e", e=PARITIES))
 
-        w_sb = consts.tile([P, PARITIES * K], BF16)
-        nc.sync.dma_start(out=w_sb[:], in_=ffn2_w.rearrange("(q e) k -> q (e k)", e=PARITIES))
-
         tiles = {}
 
-        def load(n):
+        def h_source(n):
+            rows = h_rows[n * LOAD * IMAGE : (n + 1) * LOAD * IMAGE, :]
+            return rows.rearrange("(b p t) k -> p b (t k)", b=LOAD, t=TILES)
+
+        def load_h(n):
             h_sb = h_pool.tile([P, LOAD, TILES * K], BF16, name="h_sb")
-            source = h_rows[n * LOAD * IMAGE : (n + 1) * LOAD * IMAGE, :].rearrange(
-                "(b p t) k -> p b (t k)", b=LOAD, t=TILES
-            )
-            if n == 0:
-                for b in range(LOAD):
-                    for t in range(TILES):
-                        nc.sync.dma_start(
-                            out=h_sb[:, b, t * K : (t + 1) * K], in_=source[:, b, t * K : (t + 1) * K]
-                        )
-            else:
-                nc.sync.dma_start(out=h_sb[:], in_=source)
+            nc.sync.dma_start(out=h_sb[:], in_=h_source(n))
             tiles["h", n] = h_sb
+
+        def load_x(n):
             x_sb = x_pool.tile([P, LOAD, PARITIES, IMAGE], BF16, name="x_sb")
             nc.sync.dma_start(
                 out=x_sb[:].rearrange("q b e s -> q b (e s)"),
@@ -105,8 +100,32 @@ def tile_transformerconvblock_pc_t_kernel(
             )
             tiles["x", n] = x_sb
 
-        for n in range(PREFETCH):
-            load(n)
+        first_h = h_pool.tile([P, LOAD, TILES * K], BF16, name="h_sb")
+        tiles["h", 0] = first_h
+        w_sb = consts.tile([P, PARITIES * K], BF16)
+        for b in range(LOAD):
+            for t in range(TILES):
+                cols = slice(t * K, (t + 1) * K)
+                nc.sync.dma_start(out=first_h[:, b, cols], in_=h_source(0)[:, b, cols])
+            if b == 0:
+                nc.sync.dma_start(out=w_sb[:], in_=ffn2_w.rearrange("(q e) k -> q (e k)", e=PARITIES))
+        for n in range(1, PREFETCH):
+            load_h(n)
+        for n in range(X_PREFETCH):
+            load_x(n)
+
+        def transpose_in(i):
+            n, b = divmod(i, LOAD)
+            grouped = mx_pool.tile([P, TILES * K], BF16, name="h_grouped", align_bytes=64)
+            h_words = tiles["h", n][:, b, :].bitcast(F32)
+            grouped_words = grouped[:].bitcast(F32).rearrange("p (t g c u) -> p t g c u", t=TILES, g=PASSES, u=2)
+            for t in range(TILES):
+                h_bank = in_banks.tile([P, BLOCKS, P], F32, tag="in_bank")
+                transpose_words(nc, h_bank, h_words[:, t * WORDS : (t + 1) * WORDS], ident)
+                nc.scalar.copy(out=grouped_words[:, t, :, :, :], in_=words_by_column(h_bank))
+            tiles["grouped", i] = grouped
+
+        transpose_in(0)
 
         w_words = w_sb[:].bitcast(F32)
         w_grouped = consts.tile([P, PASSES * C * 4], BF16, align_bytes=64)
@@ -143,17 +162,6 @@ def tile_transformerconvblock_pc_t_kernel(
         shift = consts.tile([P, PARITIES], F32)
         nc.vector.tensor_scalar(out=shift[:], in0=ln_b[:], scalar1=n_col[:, 0:1], scalar2=None, op0=ALU.mult)
 
-        def transpose_in(i):
-            n, b = divmod(i, LOAD)
-            grouped = mx_pool.tile([P, TILES * K], BF16, name="h_grouped", align_bytes=64)
-            h_words = tiles["h", n][:, b, :].bitcast(F32)
-            grouped_words = grouped[:].bitcast(F32).rearrange("p (t g c u) -> p t g c u", t=TILES, g=PASSES, u=2)
-            for t in range(TILES):
-                h_bank = in_banks.tile([P, BLOCKS, P], F32, tag="in_bank")
-                transpose_words(nc, h_bank, h_words[:, t * WORDS : (t + 1) * WORDS], ident)
-                nc.scalar.copy(out=grouped_words[:, t, :, :, :], in_=words_by_column(h_bank))
-            tiles["grouped", i] = grouped
-
         def quantise(i):
             codes = mx_pool.tile([P, TILES * PASSES * P], U32, name="h_codes", align_bytes=64)
             scales = mx_pool.tile([P, TILES * PASSES * P], U8, name="h_scales", align_bytes=64)
@@ -179,155 +187,135 @@ def tile_transformerconvblock_pc_t_kernel(
             tiles["acc", i] = acc
 
         def add_bias(i):
-            acc = tiles["acc", i]
+            n, b = divmod(i, LOAD)
+            if b == 0:
+                tiles["v_sum", n] = stats.tile([P, LOAD, TILES], F32, name="v_sum")
             v = work.tile([P, TILES, C], F32, name="v")
-            v_sum = stats.tile([P, TILES], F32, name="v_sum")
             for t in range(TILES):
                 nc.vector.scalar_tensor_tensor(
                     out=v[:, t, :],
-                    in0=acc[:, t, :],
+                    in0=tiles["acc", i][:, t, :],
                     scalar=1.0,
                     in1=bias_bc[:],
                     op0=ALU.mult,
                     op1=ALU.add,
-                    accum_out=v_sum[:, t : t + 1],
+                    accum_out=tiles["v_sum", n][:, b, t : t + 1],
                 )
             tiles["v", i] = v
-            tiles["v_sum", i] = v_sum
-
-        def mean(i):
-            neg_mean = stats.tile([P, TILES], F32, name="neg_mean")
-            nc.gpsimd.tensor_scalar(
-                out=neg_mean[:], in0=tiles["v_sum", i][:], scalar1=-1.0 / C, scalar2=None, op0=ALU.mult
-            )
-            tiles["neg_mean", i] = neg_mean
 
         def squares(i):
-            v = tiles["v", i]
-            v_sum = tiles["v_sum", i]
+            n, b = divmod(i, LOAD)
+            if b == 0:
+                tiles["sq_sum", n] = stats.tile([P, LOAD, TILES], F32, name="sq_sum")
             squared = work.tile([P, TILES, C], F32, name="squared")
-            sq_sum = stats.tile([P, TILES], F32, name="sq_sum")
             for t in range(TILES):
                 nc.scalar.activation(
                     out=squared[:, t, :],
-                    in_=v[:, t, :],
+                    in_=tiles["v", i][:, t, :],
                     func=ACT.Square,
-                    bias=v_sum[:, t : t + 1],
+                    bias=tiles["v_sum", n][:, b, t : t + 1],
                     scale=-float(C),
-                    accum_out=sq_sum[:, t : t + 1],
+                    accum_out=tiles["sq_sum", n][:, b, t : t + 1],
                 )
-            tiles["sq_sum", i] = sq_sum
 
-        def inverse_std(i):
-            rstd = stats.tile([P, TILES], F32, name="rstd")
+        def mean(n):
+            neg_mean = stats.tile([P, LOAD, TILES], F32, name="neg_mean")
+            nc.vector.tensor_scalar(
+                out=neg_mean[:], in0=tiles["v_sum", n][:], scalar1=-1.0 / C, scalar2=None, op0=ALU.mult
+            )
+            tiles["neg_mean", n] = neg_mean
+
+        def inverse_std(n):
+            rstd = stats.tile([P, LOAD, TILES], F32, name="rstd")
             nc.scalar.activation(
                 out=rstd[:],
-                in_=tiles["sq_sum", i][:],
+                in_=tiles["sq_sum", n][:],
                 func=ACT.Abs_reciprocal_sqrt,
                 bias=eps_col[:, 0:1],
                 scale=var_scale[:, 0:1],
             )
-            tiles["rstd", i] = rstd
-
-        def offsets(i):
-            offset = stats.tile([P, TILES], F32, name="offset")
-            nc.gpsimd.tensor_tensor(
-                out=offset[:], in0=tiles["neg_mean", i][:], in1=tiles["rstd", i][:], op=ALU.mult
-            )
-            tiles["offset", i] = offset
+            tiles["rstd", n] = rstd
 
         def normalise(i):
+            n, b = divmod(i, LOAD)
             normed = work.tile([P, TILES, C], F32, name="normed")
             for t in range(TILES):
-                nc.gpsimd.tensor_scalar(
+                nc.vector.tensor_scalar(
                     out=normed[:, t, :],
                     in0=tiles["v", i][:, t, :],
-                    scalar1=tiles["rstd", i][:, t : t + 1],
-                    scalar2=tiles["offset", i][:, t : t + 1],
-                    op0=ALU.mult,
-                    op1=ALU.add,
+                    scalar1=tiles["neg_mean", n][:, b, t : t + 1],
+                    scalar2=tiles["rstd", n][:, b, t : t + 1],
+                    op0=ALU.add,
+                    op1=ALU.mult,
                 )
             tiles["normed", i] = normed
 
-        def transpose_out(i):
-            o_bank = out_banks.tile([P, PARITIES, TILES, P], F32, tag="out_bank")
-            for e in range(PARITIES):
+        def transpose_out(n, e):
+            o_bank = out_banks.tile([P, TILES, LOAD, P], F32, tag="out_bank")
+            for b in range(LOAD):
                 for t in range(TILES):
-                    nc.tensor.transpose(o_bank[:, e, t, :], tiles["normed", i][:, t, e * P : (e + 1) * P], ident[:])
-            tiles["o_bank", i] = o_bank
+                    nc.tensor.transpose(
+                        o_bank[:, t, b, :], tiles["normed", n * LOAD + b][:, t, e * P : (e + 1) * P], ident[:]
+                    )
+            tiles["o_bank", n, e] = o_bank
 
-        def add_x(i):
-            n, b = divmod(i, LOAD)
-            o_sb = work.tile([P, PARITIES, IMAGE], F32, name="o_sb", bufs=6)
-            for e in range(PARITIES):
-                nc.vector.scalar_tensor_tensor(
-                    out=o_sb[:, e, :].rearrange("q (p t) -> q p t", t=TILES),
-                    in0=tiles["o_bank", i][:, e, :, :].rearrange("q t p -> q p t"),
-                    scalar=gain[:, e : e + 1],
-                    in1=tiles["x", n][:, b, e, :].rearrange("q (p t) -> q p t", t=TILES),
-                    op0=ALU.mult,
-                    op1=ALU.add,
-                )
-            tiles["o", i] = o_sb
+        def add_x(n, e):
+            if e == 0:
+                tiles["o", n] = work.tile([P, LOAD, PARITIES, IMAGE], F32, name="o_sb", bufs=4)
+            nc.vector.scalar_tensor_tensor(
+                out=tiles["o", n][:, :, e, :].rearrange("q b (p t) -> q b p t", t=TILES),
+                in0=tiles["o_bank", n, e][:].rearrange("q t b p -> q b p t"),
+                scalar=gain[:, e : e + 1],
+                in1=tiles["x", n][:, :, e, :].rearrange("q b (p t) -> q b p t", t=TILES),
+                op0=ALU.mult,
+                op1=ALU.add,
+            )
 
-        def relu_on_vector(i):
-            for e in range(SPLIT):
+        def relu(n, e):
+            half = tiles["o", n][:, :, e, :]
+            if e < ON_VECTOR:
                 nc.vector.tensor_scalar(
-                    out=tiles["o", i][:, e, :],
-                    in0=tiles["o", i][:, e, :],
-                    scalar1=shift[:, e : e + 1],
-                    scalar2=0.0,
-                    op0=ALU.add,
-                    op1=ALU.max,
+                    out=half, in0=half, scalar1=shift[:, e : e + 1], scalar2=0.0, op0=ALU.add, op1=ALU.max
                 )
+            else:
+                nc.scalar.activation(out=half, in_=half, func=ACT.Relu, bias=shift[:, e : e + 1], scale=1.0)
 
-        def relu_on_scalar(i):
-            for e in range(SPLIT, PARITIES):
-                nc.scalar.activation(
-                    out=tiles["o", i][:, e, :],
-                    in_=tiles["o", i][:, e, :],
-                    func=ACT.Relu,
-                    bias=shift[:, e : e + 1],
-                    scale=1.0,
-                )
-
-        def store(i):
+        def store(n):
             nc.sync.dma_start(
-                out=out[i].rearrange("(q e) i j -> q (e i j)", e=PARITIES),
-                in_=tiles["o", i][:].rearrange("q e s -> q (e s)"),
+                out=out[n * LOAD : (n + 1) * LOAD].rearrange("b (q e) i j -> q b (e i j)", e=PARITIES),
+                in_=tiles["o", n][:].rearrange("q b e s -> q b (e s)"),
             )
 
         def is_image(i):
             return 0 <= i < IMAGES
 
-        for step in range(IMAGES + 7):
-            if step % LOAD == 0 and step // LOAD + PREFETCH < IMAGES // LOAD:
-                load(step // LOAD + PREFETCH)
-            if is_image(step):
-                transpose_in(step)
-            if is_image(step - 2):
-                squares(step - 2)
-            if is_image(step - 5):
-                transpose_out(step - 5)
-            if is_image(step - 6):
-                relu_on_scalar(step - 6)
-            if is_image(step - 5):
-                add_x(step - 5)
-            if is_image(step - 3):
-                mean(step - 3)
-            if is_image(step - 2):
-                inverse_std(step - 2)
-            if is_image(step - 5):
-                relu_on_vector(step - 5)
-            if is_image(step - 3):
-                offsets(step - 3)
-            if is_image(step):
-                quantise(step)
-            if is_image(step - 3):
-                normalise(step - 3)
+        for step in range(IMAGES + 9):
+            if step % LOAD == 0:
+                if step // LOAD + PREFETCH < LOADS:
+                    load_h(step // LOAD + PREFETCH)
+                if step // LOAD + X_PREFETCH < LOADS:
+                    load_x(step // LOAD + X_PREFETCH)
+            if is_image(step + 1):
+                transpose_in(step + 1)
             if is_image(step - 1):
                 multiply(step - 1)
             if is_image(step - 6):
-                store(step - 6)
+                transpose_out(*divmod(step - 6, LOAD))
+            if is_image(step - 2):
+                squares(step - 2)
+            if is_image(step - 8):
+                relu(*divmod(step - 8, LOAD))
+            if is_image(step - 2) and (step - 2) % LOAD == LOAD - 1:
+                inverse_std((step - 2) // LOAD)
+            if is_image(step - 8) and (step - 8) % LOAD == LOAD - 1:
+                store((step - 8) // LOAD)
+            if is_image(step - 2) and (step - 2) % LOAD == LOAD - 1:
+                mean((step - 2) // LOAD)
+            if is_image(step):
+                quantise(step)
             if is_image(step - 1):
                 add_bias(step - 1)
+            if is_image(step - 4):
+                normalise(step - 4)
+            if is_image(step - 6):
+                add_x(*divmod(step - 6, LOAD))

@@ -23,7 +23,6 @@ WORDS = K // 2
 BLOCKS = WORDS // P
 PARITIES = C // P
 TILES = IMAGE // P
-ON_VECTOR = 0
 LOAD = 2
 LOADS = IMAGES // LOAD
 PREFETCH = 4
@@ -60,18 +59,10 @@ def tile_transformerconvblock_pc_t_kernel(
         out_banks = ctx.enter_context(tc.psum_pool(name="out_banks", bufs=2))
         ctx.enter_context(tc.manual_schedule())
 
-        ident = consts.tile([P, P], F32)
-        make_identity(nc, ident[:])
-        ones = consts.tile([P, P], BF16)
-        nc.vector.memset(ones[:], 1.0)
-        eps_col = consts.tile([P, 1], F32)
-        nc.vector.tensor_scalar(out=eps_col[:], in0=ones[:, 0:1], scalar1=EPS, scalar2=None, op0=ALU.mult)
-        warm = consts.tile([P, 1], F32)
-        nc.scalar.activation(out=warm[:], in_=eps_col[:], func=ACT.Abs_reciprocal_sqrt)
-
         S_AT = C
         N_AT = C + 16
-        row = consts.tile([P, 512], BF16)
+        ROW = C + 32
+        row = consts.tile([P, ROW], BF16)
         nc.vector.memset(row[:], 0.0)
         nc.scalar.dma_start(out=row[0:1, 0:C], in_=ffn2_b.rearrange("(o c) -> o c", o=1))
         nc.scalar.dma_start(out=row[0:1, S_AT : S_AT + 1], in_=scale_ffn.rearrange("(o c) -> o c", o=1))
@@ -80,6 +71,14 @@ def tile_transformerconvblock_pc_t_kernel(
         nc.scalar.dma_start(out=ln_w[:], in_=ln2_w.rearrange("(q e) -> q e", e=PARITIES))
         ln_b = consts.tile([P, PARITIES], BF16)
         nc.scalar.dma_start(out=ln_b[:], in_=ln2_b.rearrange("(q e) -> q e", e=PARITIES))
+        ident = consts.tile([P, P], F32)
+        make_identity(nc, ident[:])
+        ones = consts.tile([P, P], BF16)
+        nc.vector.memset(ones[:], 1.0)
+        eps_col = consts.tile([P, 1], F32)
+        nc.vector.tensor_scalar(out=eps_col[:], in0=ones[:, 0:1], scalar1=EPS, scalar2=None, op0=ALU.mult)
+        warm = consts.tile([P, 1], F32)
+        nc.scalar.activation(out=warm[:], in_=eps_col[:], func=ACT.Abs_reciprocal_sqrt)
 
         tiles = {}
 
@@ -100,47 +99,57 @@ def tile_transformerconvblock_pc_t_kernel(
             )
             tiles["x", n] = x_sb
 
+        w_sb = consts.tile([P, PARITIES, K], BF16)
         first_h = h_pool.tile([P, LOAD, TILES * K], BF16, name="h_sb")
         tiles["h", 0] = first_h
-        w_sb = consts.tile([P, PARITIES * K], BF16)
-        for b in range(LOAD):
-            for t in range(TILES):
-                cols = slice(t * K, (t + 1) * K)
-                nc.sync.dma_start(out=first_h[:, b, cols], in_=h_source(0)[:, b, cols])
-            if b == 0:
-                nc.sync.dma_start(out=w_sb[:], in_=ffn2_w.rearrange("(q e) k -> q (e k)", e=PARITIES))
+        w_source = ffn2_w.rearrange("(q e) k -> q e k", e=PARITIES)
+        for j in range(PARITIES):
+            nc.sync.dma_start(out=w_sb[:, j, :], in_=w_source[:, j, :])
+            cols = slice(j * K, (j + 1) * K)
+            nc.sync.dma_start(out=first_h[:, 0, cols], in_=h_source(0)[:, 0, cols])
+        nc.sync.dma_start(out=first_h[:, 1, :], in_=h_source(0)[:, 1, :])
         for n in range(1, PREFETCH):
             load_h(n)
         for n in range(X_PREFETCH):
             load_x(n)
 
-        def transpose_in(i):
+        def transpose_tile(i, t):
             n, b = divmod(i, LOAD)
-            grouped = mx_pool.tile([P, TILES * K], BF16, name="h_grouped", align_bytes=64)
+            if t == 0:
+                tiles["grouped", i] = mx_pool.tile([P, TILES * K], BF16, name="h_grouped", align_bytes=64)
+            grouped_words = tiles["grouped", i][:].bitcast(F32).rearrange(
+                "p (t g c u) -> p t g c u", t=TILES, g=PASSES, u=2
+            )
             h_words = tiles["h", n][:, b, :].bitcast(F32)
-            grouped_words = grouped[:].bitcast(F32).rearrange("p (t g c u) -> p t g c u", t=TILES, g=PASSES, u=2)
+            h_bank = in_banks.tile([P, BLOCKS, P], F32, tag="in_bank")
+            transpose_words(nc, h_bank, h_words[:, t * WORDS : (t + 1) * WORDS], ident)
+            nc.scalar.copy(out=grouped_words[:, t, :, :, :], in_=words_by_column(h_bank))
+
+        def transpose_in(i):
             for t in range(TILES):
-                h_bank = in_banks.tile([P, BLOCKS, P], F32, tag="in_bank")
-                transpose_words(nc, h_bank, h_words[:, t * WORDS : (t + 1) * WORDS], ident)
-                nc.scalar.copy(out=grouped_words[:, t, :, :, :], in_=words_by_column(h_bank))
-            tiles["grouped", i] = grouped
+                transpose_tile(i, t)
 
-        transpose_in(0)
+        def quantise(i):
+            codes = mx_pool.tile([P, TILES * PASSES * P], U32, name="h_codes", align_bytes=64)
+            scales = mx_pool.tile([P, TILES * PASSES * P], U8, name="h_scales", align_bytes=64)
+            nc.vector.quantize_mx(out=codes[:].bitcast(FP8X4), scales=scales[:], in_=tiles["grouped", i][:])
+            tiles["mx", i] = codes, scales
 
-        w_words = w_sb[:].bitcast(F32)
         w_grouped = consts.tile([P, PASSES * C * 4], BF16, align_bytes=64)
         w_grouped_words = w_grouped[:].bitcast(F32).rearrange(
             "p (g e q u) -> p g e q u", g=PASSES, e=PARITIES, u=2
         )
-        for e in range(PARITIES):
+        for j in range(PARITIES):
             w_bank = in_banks.tile([P, BLOCKS, P], F32, tag="in_bank")
-            transpose_words(nc, w_bank, w_words[:, e * WORDS : (e + 1) * WORDS], ident)
-            nc.vector.tensor_copy(out=w_grouped_words[:, :, e, :, :], in_=words_by_column(w_bank))
+            transpose_words(nc, w_bank, w_sb[:, j, :].bitcast(F32), ident)
+            nc.vector.tensor_copy(out=w_grouped_words[:, :, j, :, :], in_=words_by_column(w_bank))
+            transpose_tile(0, j)
         w_codes = consts.tile([P, PASSES * C], U32, align_bytes=64)
         w_scales = consts.tile([P, PASSES * C], U8, align_bytes=64)
         nc.vector.quantize_mx(out=w_codes[:].bitcast(FP8X4), scales=w_scales[:], in_=w_grouped[:])
+        quantise(0)
 
-        row_bank = out_banks.tile([P, 512], F32, tag="out_bank")
+        row_bank = out_banks.tile([P, ROW], F32, tag="out_bank")
         nc.tensor.matmul(out=row_bank[:], lhsT=ones[:], rhs=row[:], start=True, stop=True)
         bias_bc = consts.tile([P, C], F32)
         nc.vector.tensor_copy(
@@ -161,12 +170,8 @@ def tile_transformerconvblock_pc_t_kernel(
         )
         shift = consts.tile([P, PARITIES], F32)
         nc.vector.tensor_scalar(out=shift[:], in0=ln_b[:], scalar1=n_col[:, 0:1], scalar2=None, op0=ALU.mult)
-
-        def quantise(i):
-            codes = mx_pool.tile([P, TILES * PASSES * P], U32, name="h_codes", align_bytes=64)
-            scales = mx_pool.tile([P, TILES * PASSES * P], U8, name="h_scales", align_bytes=64)
-            nc.vector.quantize_mx(out=codes[:].bitcast(FP8X4), scales=scales[:], in_=tiles["grouped", i][:])
-            tiles["mx", i] = codes, scales
+        transpose_in(1)
+        quantise(1)
 
         def multiply(i):
             codes, scales = tiles["mx", i]
@@ -187,10 +192,8 @@ def tile_transformerconvblock_pc_t_kernel(
             tiles["acc", i] = acc
 
         def add_bias(i):
-            n, b = divmod(i, LOAD)
-            if b == 0:
-                tiles["v_sum", n] = stats.tile([P, LOAD, TILES], F32, name="v_sum")
             v = work.tile([P, TILES, C], F32, name="v")
+            v_sum = stats.tile([P, TILES], F32, name="v_sum")
             for t in range(TILES):
                 nc.vector.scalar_tensor_tensor(
                     out=v[:, t, :],
@@ -199,52 +202,51 @@ def tile_transformerconvblock_pc_t_kernel(
                     in1=bias_bc[:],
                     op0=ALU.mult,
                     op1=ALU.add,
-                    accum_out=tiles["v_sum", n][:, b, t : t + 1],
+                    accum_out=v_sum[:, t : t + 1],
                 )
             tiles["v", i] = v
+            tiles["v_sum", i] = v_sum
 
         def squares(i):
-            n, b = divmod(i, LOAD)
-            if b == 0:
-                tiles["sq_sum", n] = stats.tile([P, LOAD, TILES], F32, name="sq_sum")
             squared = work.tile([P, TILES, C], F32, name="squared")
+            sq_sum = stats.tile([P, TILES], F32, name="sq_sum")
             for t in range(TILES):
                 nc.scalar.activation(
                     out=squared[:, t, :],
                     in_=tiles["v", i][:, t, :],
                     func=ACT.Square,
-                    bias=tiles["v_sum", n][:, b, t : t + 1],
+                    bias=tiles["v_sum", i][:, t : t + 1],
                     scale=-float(C),
-                    accum_out=tiles["sq_sum", n][:, b, t : t + 1],
+                    accum_out=sq_sum[:, t : t + 1],
                 )
+            tiles["sq_sum", i] = sq_sum
 
-        def mean(n):
-            neg_mean = stats.tile([P, LOAD, TILES], F32, name="neg_mean")
-            nc.vector.tensor_scalar(
-                out=neg_mean[:], in0=tiles["v_sum", n][:], scalar1=-1.0 / C, scalar2=None, op0=ALU.mult
+        def mean(i):
+            neg_mean = stats.tile([P, TILES], F32, name="neg_mean")
+            nc.gpsimd.tensor_scalar(
+                out=neg_mean[:], in0=tiles["v_sum", i][:], scalar1=-1.0 / C, scalar2=0.0, op0=ALU.mult, op1=ALU.add
             )
-            tiles["neg_mean", n] = neg_mean
+            tiles["neg_mean", i] = neg_mean
 
-        def inverse_std(n):
-            rstd = stats.tile([P, LOAD, TILES], F32, name="rstd")
+        def inverse_std(i):
+            rstd = stats.tile([P, TILES], F32, name="rstd")
             nc.scalar.activation(
                 out=rstd[:],
-                in_=tiles["sq_sum", n][:],
+                in_=tiles["sq_sum", i][:],
                 func=ACT.Abs_reciprocal_sqrt,
                 bias=eps_col[:, 0:1],
                 scale=var_scale[:, 0:1],
             )
-            tiles["rstd", n] = rstd
+            tiles["rstd", i] = rstd
 
         def normalise(i):
-            n, b = divmod(i, LOAD)
             normed = work.tile([P, TILES, C], F32, name="normed")
             for t in range(TILES):
-                nc.vector.tensor_scalar(
+                nc.gpsimd.tensor_scalar(
                     out=normed[:, t, :],
                     in0=tiles["v", i][:, t, :],
-                    scalar1=tiles["neg_mean", n][:, b, t : t + 1],
-                    scalar2=tiles["rstd", n][:, b, t : t + 1],
+                    scalar1=tiles["neg_mean", i][:, t : t + 1],
+                    scalar2=tiles["rstd", i][:, t : t + 1],
                     op0=ALU.add,
                     op1=ALU.mult,
                 )
@@ -273,7 +275,7 @@ def tile_transformerconvblock_pc_t_kernel(
 
         def relu(n, e):
             half = tiles["o", n][:, :, e, :]
-            if e < ON_VECTOR:
+            if e == 0:
                 nc.vector.tensor_scalar(
                     out=half, in0=half, scalar1=shift[:, e : e + 1], scalar2=0.0, op0=ALU.add, op1=ALU.max
                 )
@@ -289,33 +291,33 @@ def tile_transformerconvblock_pc_t_kernel(
         def is_image(i):
             return 0 <= i < IMAGES
 
-        for step in range(IMAGES + 9):
+        for step in range(IMAGES + 8):
             if step % LOAD == 0:
                 if step // LOAD + PREFETCH < LOADS:
                     load_h(step // LOAD + PREFETCH)
                 if step // LOAD + X_PREFETCH < LOADS:
                     load_x(step // LOAD + X_PREFETCH)
-            if is_image(step + 1):
-                transpose_in(step + 1)
             if is_image(step - 1):
-                multiply(step - 1)
-            if is_image(step - 6):
-                transpose_out(*divmod(step - 6, LOAD))
-            if is_image(step - 2):
-                squares(step - 2)
-            if is_image(step - 8):
-                relu(*divmod(step - 8, LOAD))
-            if is_image(step - 2) and (step - 2) % LOAD == LOAD - 1:
-                inverse_std((step - 2) // LOAD)
-            if is_image(step - 8) and (step - 8) % LOAD == LOAD - 1:
-                store((step - 8) // LOAD)
-            if is_image(step - 2) and (step - 2) % LOAD == LOAD - 1:
-                mean((step - 2) // LOAD)
+                squares(step - 1)
+            if is_image(step + 2):
+                transpose_in(step + 2)
             if is_image(step):
-                quantise(step)
-            if is_image(step - 1):
-                add_bias(step - 1)
+                multiply(step)
             if is_image(step - 4):
-                normalise(step - 4)
+                transpose_out(*divmod(step - 4, LOAD))
+            if is_image(step - 1):
+                inverse_std(step - 1)
+            if is_image(step):
+                add_bias(step)
             if is_image(step - 6):
-                add_x(*divmod(step - 6, LOAD))
+                relu(*divmod(step - 6, LOAD))
+            if is_image(step - 4):
+                add_x(*divmod(step - 4, LOAD))
+            if is_image(step + 2):
+                quantise(step + 2)
+            if is_image(step - 1):
+                mean(step - 1)
+            if is_image(step - 2):
+                normalise(step - 2)
+            if is_image(step - 7) and (step - 7) % LOAD == LOAD - 1:
+                store((step - 7) // LOAD)

@@ -59,27 +59,6 @@ def tile_transformerconvblock_pc_t_kernel(
         out_banks = ctx.enter_context(tc.psum_pool(name="out_banks", bufs=2))
         ctx.enter_context(tc.manual_schedule())
 
-        S_AT = C
-        N_AT = C + 16
-        ROW = C + 32
-        row = consts.tile([P, ROW], BF16)
-        nc.vector.memset(row[:], 0.0)
-        nc.scalar.dma_start(out=row[0:1, 0:C], in_=ffn2_b.rearrange("(o c) -> o c", o=1))
-        nc.scalar.dma_start(out=row[0:1, S_AT : S_AT + 1], in_=scale_ffn.rearrange("(o c) -> o c", o=1))
-        nc.scalar.dma_start(out=row[0:1, N_AT : N_AT + 1], in_=scale_norm2.rearrange("(o c) -> o c", o=1))
-        ln_w = consts.tile([P, PARITIES], BF16)
-        nc.scalar.dma_start(out=ln_w[:], in_=ln2_w.rearrange("(q e) -> q e", e=PARITIES))
-        ln_b = consts.tile([P, PARITIES], BF16)
-        nc.scalar.dma_start(out=ln_b[:], in_=ln2_b.rearrange("(q e) -> q e", e=PARITIES))
-        ident = consts.tile([P, P], F32)
-        make_identity(nc, ident[:])
-        ones = consts.tile([P, P], BF16)
-        nc.vector.memset(ones[:], 1.0)
-        eps_col = consts.tile([P, 1], F32)
-        nc.vector.tensor_scalar(out=eps_col[:], in0=ones[:, 0:1], scalar1=EPS, scalar2=None, op0=ALU.mult)
-        warm = consts.tile([P, 1], F32)
-        nc.scalar.activation(out=warm[:], in_=eps_col[:], func=ACT.Abs_reciprocal_sqrt)
-
         tiles = {}
 
         def h_source(n):
@@ -88,8 +67,12 @@ def tile_transformerconvblock_pc_t_kernel(
 
         def load_h(n):
             h_sb = h_pool.tile([P, LOAD, TILES * K], BF16, name="h_sb")
-            nc.sync.dma_start(out=h_sb[:], in_=h_source(n))
             tiles["h", n] = h_sb
+            if n <= 1:
+                for b in range(LOAD):
+                    nc.sync.dma_start(out=h_sb[:, b, :], in_=h_source(n)[:, b, :])
+            else:
+                nc.sync.dma_start(out=h_sb[:], in_=h_source(n))
 
         def load_x(n):
             x_sb = x_pool.tile([P, LOAD, PARITIES, IMAGE], BF16, name="x_sb")
@@ -107,11 +90,33 @@ def tile_transformerconvblock_pc_t_kernel(
             nc.sync.dma_start(out=w_sb[:, j, :], in_=w_source[:, j, :])
             cols = slice(j * K, (j + 1) * K)
             nc.sync.dma_start(out=first_h[:, 0, cols], in_=h_source(0)[:, 0, cols])
+
+        S_AT = C
+        N_AT = C + 16
+        ROW = C + 32
+        row = consts.tile([P, ROW], BF16)
+        nc.vector.memset(row[:], 0.0)
+        nc.scalar.dma_start(out=row[0:1, 0:C], in_=ffn2_b.rearrange("(o c) -> o c", o=1))
+        nc.scalar.dma_start(out=row[0:1, S_AT : S_AT + 1], in_=scale_ffn.rearrange("(o c) -> o c", o=1))
+        nc.scalar.dma_start(out=row[0:1, N_AT : N_AT + 1], in_=scale_norm2.rearrange("(o c) -> o c", o=1))
         nc.sync.dma_start(out=first_h[:, 1, :], in_=h_source(0)[:, 1, :])
-        for n in range(1, PREFETCH):
+        load_h(1)
+        ln_w = consts.tile([P, PARITIES], BF16)
+        nc.sync.dma_start(out=ln_w[:], in_=ln2_w.rearrange("(q e) -> q e", e=PARITIES))
+        ln_b = consts.tile([P, PARITIES], BF16)
+        nc.sync.dma_start(out=ln_b[:], in_=ln2_b.rearrange("(q e) -> q e", e=PARITIES))
+        for n in range(2, PREFETCH):
             load_h(n)
         for n in range(X_PREFETCH):
             load_x(n)
+        ident = consts.tile([P, P], F32)
+        make_identity(nc, ident[:])
+        ones = consts.tile([P, P], BF16)
+        nc.vector.memset(ones[:], 1.0)
+        eps_col = consts.tile([P, 1], F32)
+        nc.vector.tensor_scalar(out=eps_col[:], in0=ones[:, 0:1], scalar1=EPS, scalar2=None, op0=ALU.mult)
+        warm = consts.tile([P, 1], F32)
+        nc.scalar.activation(out=warm[:], in_=eps_col[:], func=ACT.Abs_reciprocal_sqrt)
 
         def transpose_tile(i, t):
             n, b = divmod(i, LOAD)
@@ -192,8 +197,10 @@ def tile_transformerconvblock_pc_t_kernel(
             tiles["acc", i] = acc
 
         def add_bias(i):
+            n, b = divmod(i, LOAD)
+            if b == 0:
+                tiles["v_sum", n] = stats.tile([P, LOAD, TILES], F32, name="v_sum")
             v = work.tile([P, TILES, C], F32, name="v")
-            v_sum = stats.tile([P, TILES], F32, name="v_sum")
             for t in range(TILES):
                 nc.vector.scalar_tensor_tensor(
                     out=v[:, t, :],
@@ -202,12 +209,12 @@ def tile_transformerconvblock_pc_t_kernel(
                     in1=bias_bc[:],
                     op0=ALU.mult,
                     op1=ALU.add,
-                    accum_out=v_sum[:, t : t + 1],
+                    accum_out=tiles["v_sum", n][:, b, t : t + 1],
                 )
             tiles["v", i] = v
-            tiles["v_sum", i] = v_sum
 
         def squares(i):
+            n, b = divmod(i, LOAD)
             squared = work.tile([P, TILES, C], F32, name="squared")
             sq_sum = stats.tile([P, TILES], F32, name="sq_sum")
             for t in range(TILES):
@@ -215,18 +222,18 @@ def tile_transformerconvblock_pc_t_kernel(
                     out=squared[:, t, :],
                     in_=tiles["v", i][:, t, :],
                     func=ACT.Square,
-                    bias=tiles["v_sum", i][:, t : t + 1],
+                    bias=tiles["v_sum", n][:, b, t : t + 1],
                     scale=-float(C),
                     accum_out=sq_sum[:, t : t + 1],
                 )
             tiles["sq_sum", i] = sq_sum
 
-        def mean(i):
-            neg_mean = stats.tile([P, TILES], F32, name="neg_mean")
-            nc.gpsimd.tensor_scalar(
-                out=neg_mean[:], in0=tiles["v_sum", i][:], scalar1=-1.0 / C, scalar2=0.0, op0=ALU.mult, op1=ALU.add
+        def mean(n):
+            neg_mean = stats.tile([P, LOAD, TILES], F32, name="neg_mean")
+            nc.vector.tensor_scalar(
+                out=neg_mean[:], in0=tiles["v_sum", n][:], scalar1=-1.0 / C, scalar2=None, op0=ALU.mult
             )
-            tiles["neg_mean", i] = neg_mean
+            tiles["neg_mean", n] = neg_mean
 
         def inverse_std(i):
             rstd = stats.tile([P, TILES], F32, name="rstd")
@@ -238,19 +245,18 @@ def tile_transformerconvblock_pc_t_kernel(
                 scale=var_scale[:, 0:1],
             )
             tiles["rstd", i] = rstd
+            tiles["normed", i] = work.tile([P, TILES, C], F32, name="normed")
 
-        def normalise(i):
-            normed = work.tile([P, TILES, C], F32, name="normed")
-            for t in range(TILES):
-                nc.gpsimd.tensor_scalar(
-                    out=normed[:, t, :],
-                    in0=tiles["v", i][:, t, :],
-                    scalar1=tiles["neg_mean", i][:, t : t + 1],
-                    scalar2=tiles["rstd", i][:, t : t + 1],
-                    op0=ALU.add,
-                    op1=ALU.mult,
-                )
-            tiles["normed", i] = normed
+        def normalise(engine, i, t):
+            n, b = divmod(i, LOAD)
+            engine.tensor_scalar(
+                out=tiles["normed", i][:, t, :],
+                in0=tiles["v", i][:, t, :],
+                scalar1=tiles["neg_mean", n][:, b, t : t + 1],
+                scalar2=tiles["rstd", i][:, t : t + 1],
+                op0=ALU.add,
+                op1=ALU.mult,
+            )
 
         def transpose_out(n, e):
             o_bank = out_banks.tile([P, TILES, LOAD, P], F32, tag="out_bank")
@@ -275,7 +281,7 @@ def tile_transformerconvblock_pc_t_kernel(
 
         def relu(n, e):
             half = tiles["o", n][:, :, e, :]
-            if e == 0:
+            if n % 2 == 0 and e == 0:
                 nc.vector.tensor_scalar(
                     out=half, in0=half, scalar1=shift[:, e : e + 1], scalar2=0.0, op0=ALU.add, op1=ALU.max
                 )
@@ -291,7 +297,7 @@ def tile_transformerconvblock_pc_t_kernel(
         def is_image(i):
             return 0 <= i < IMAGES
 
-        for step in range(IMAGES + 8):
+        for step in range(IMAGES + 9):
             if step % LOAD == 0:
                 if step // LOAD + PREFETCH < LOADS:
                     load_h(step // LOAD + PREFETCH)
@@ -303,21 +309,23 @@ def tile_transformerconvblock_pc_t_kernel(
                 transpose_in(step + 2)
             if is_image(step):
                 multiply(step)
-            if is_image(step - 4):
-                transpose_out(*divmod(step - 4, LOAD))
+            if is_image(step - 3):
+                normalise(nc.vector, step - 3, 0)
+            if is_image(step - 5):
+                transpose_out(*divmod(step - 5, LOAD))
             if is_image(step - 1):
                 inverse_std(step - 1)
             if is_image(step):
                 add_bias(step)
-            if is_image(step - 6):
-                relu(*divmod(step - 6, LOAD))
-            if is_image(step - 4):
-                add_x(*divmod(step - 4, LOAD))
+            if is_image(step - 5):
+                add_x(*divmod(step - 5, LOAD))
+            if is_image(step - 7):
+                relu(*divmod(step - 7, LOAD))
+            if is_image(step) and (step) % LOAD == LOAD - 1:
+                mean((step) // LOAD)
             if is_image(step + 2):
                 quantise(step + 2)
-            if is_image(step - 1):
-                mean(step - 1)
-            if is_image(step - 2):
-                normalise(step - 2)
-            if is_image(step - 7) and (step - 7) % LOAD == LOAD - 1:
-                store((step - 7) // LOAD)
+            if is_image(step - 3):
+                normalise(nc.gpsimd, step - 3, 1)
+            if is_image(step - 8) and (step - 8) % LOAD == LOAD - 1:
+                store((step - 8) // LOAD)

@@ -281,7 +281,7 @@ def tile_transformerconvblock_pc_t_kernel(
 
         def relu(n, e):
             half = tiles["o", n][:, :, e, :]
-            if n % 2 == 0 and e == 0:
+            if n % 4 == 2 and e == 0:
                 nc.vector.tensor_scalar(
                     out=half, in0=half, scalar1=shift[:, e : e + 1], scalar2=0.0, op0=ALU.add, op1=ALU.max
                 )

from contextlib import ExitStack

import concourse.mybir as mybir
from concourse.masks import make_identity

F32 = mybir.dt.float32
BF16 = mybir.dt.bfloat16
U32 = mybir.dt.uint32
U8 = mybir.dt.uint8
FP8X4 = mybir.dt.float8_e4m3fn_x4
ALU = mybir.AluOpType
ACT = mybir.ActivationFunctionType

P = 128
K = 1024
C = 256
IMAGES = 32
IMAGE = 16 * 16
PIXELS = IMAGES * IMAGE
EPS = 1e-5
PASSES = K // (4 * P)
WORDS = K // 2
BLOCKS = WORDS // P
PARITIES = C // P
TILES = IMAGE // P
LOAD = 2
LOADS = IMAGES // LOAD
PREFETCH = 4
X_PREFETCH = 1

FLOPS = 2 * PIXELS * K * C


def transpose_words(nc, bank, words, ident):
    for j in range(BLOCKS):
        g, u = divmod(j, 2)
        nc.tensor.transpose(bank[:, j, :], words[:, 2 * P * g + u : 2 * P * (g + 1) : 2], ident[:])


def words_by_column(bank):
    return bank[:].rearrange("p (g u) c -> p g c u", u=2)


def tile_transformerconvblock_pc_t_kernel(
    tc, h, ffn2_w, ffn2_b, scale_ffn, ln2_w, ln2_b, scale_norm2, x, out
):
    nc = tc.nc
    h_rows = h.rearrange("b i j k -> (b i j) k")

    with ExitStack() as ctx:
        consts = ctx.enter_context(tc.tile_pool(name="consts", bufs=1))
        h_pool = ctx.enter_context(tc.tile_pool(name="h_pool", bufs=6))
        x_pool = ctx.enter_context(tc.tile_pool(name="x_pool", bufs=PREFETCH + 6))
        mx_pool = ctx.enter_context(tc.tile_pool(name="mx_pool", bufs=3))
        work = ctx.enter_context(tc.tile_pool(name="work", bufs=6))
        stats = ctx.enter_context(tc.tile_pool(name="stats", bufs=5))
        in_banks = ctx.enter_context(tc.psum_pool(name="in_banks", bufs=4))
        acc_banks = ctx.enter_context(tc.psum_pool(name="acc_banks", bufs=2))
        out_banks = ctx.enter_context(tc.psum_pool(name="out_banks", bufs=2))
        ctx.enter_context(tc.manual_schedule())

        tiles = {}

        def h_source(n):
            rows = h_rows[n * LOAD * IMAGE : (n + 1) * LOAD * IMAGE, :]
            return rows.rearrange("(b p t) k -> p b (t k)", b=LOAD, t=TILES)

        def load_h(n):
            h_sb = h_pool.tile([P, LOAD, TILES * K], BF16, name="h_sb")
            tiles["h", n] = h_sb
            if n <= 1:
                for b in range(LOAD):
                    nc.sync.dma_start(out=h_sb[:, b, :], in_=h_source(n)[:, b, :])
            else:
                nc.sync.dma_start(out=h_sb[:], in_=h_source(n))

        def load_x(n):
            x_sb = x_pool.tile([P, LOAD, PARITIES, IMAGE], BF16, name="x_sb")
            nc.sync.dma_start(
                out=x_sb[:].rearrange("q b e s -> q b (e s)"),
                in_=x[n * LOAD : (n + 1) * LOAD].rearrange("b (q e) i j -> q b (e i j)", e=PARITIES),
            )
            tiles["x", n] = x_sb

        w_sb = consts.tile([P, PARITIES, K], BF16)
        first_h = h_pool.tile([P, LOAD, TILES * K], BF16, name="h_sb")
        tiles["h", 0] = first_h
        w_source = ffn2_w.rearrange("(q e) k -> q e k", e=PARITIES)
        for j in range(PARITIES):
            nc.sync.dma_start(out=w_sb[:, j, :], in_=w_source[:, j, :])
            cols = slice(j * K, (j + 1) * K)
            nc.sync.dma_start(out=first_h[:, 0, cols], in_=h_source(0)[:, 0, cols])

        S_AT = C
        N_AT = C + 16
        ROW = C + 32
        row = consts.tile([P, ROW], BF16)
        nc.vector.memset(row[:], 0.0)
        nc.scalar.dma_start(out=row[0:1, 0:C], in_=ffn2_b.rearrange("(o c) -> o c", o=1))
        nc.scalar.dma_start(out=row[0:1, S_AT : S_AT + 1], in_=scale_ffn.rearrange("(o c) -> o c", o=1))
        nc.scalar.dma_start(out=row[0:1, N_AT : N_AT + 1], in_=scale_norm2.rearrange("(o c) -> o c", o=1))
        nc.sync.dma_start(out=first_h[:, 1, :], in_=h_source(0)[:, 1, :])
        load_h(1)
        ln_w = consts.tile([P, PARITIES], BF16)
        nc.sync.dma_start(out=ln_w[:], in_=ln2_w.rearrange("(q e) -> q e", e=PARITIES))
        ln_b = consts.tile([P, PARITIES], BF16)
        nc.sync.dma_start(out=ln_b[:], in_=ln2_b.rearrange("(q e) -> q e", e=PARITIES))
        for n in range(2, PREFETCH):
            load_h(n)
        for n in range(X_PREFETCH):
            load_x(n)
        ident = consts.tile([P, P], F32)
        make_identity(nc, ident[:])
        ones = consts.tile([P, P], BF16)
        nc.vector.memset(ones[:], 1.0)
        eps_col = consts.tile([P, 1], F32)
        nc.vector.tensor_scalar(out=eps_col[:], in0=ones[:, 0:1], scalar1=EPS, scalar2=None, op0=ALU.mult)
        warm = consts.tile([P, 1], F32)
        nc.scalar.activation(out=warm[:], in_=eps_col[:], func=ACT.Abs_reciprocal_sqrt)

        def transpose_tile(i, t):
            n, b = divmod(i, LOAD)
            if t == 0:
                tiles["grouped", i] = mx_pool.tile([P, TILES * K], BF16, name="h_grouped", align_bytes=64)
            grouped_words = tiles["grouped", i][:].bitcast(F32).rearrange(
                "p (t g c u) -> p t g c u", t=TILES, g=PASSES, u=2
            )
            h_words = tiles["h", n][:, b, :].bitcast(F32)
            h_bank = in_banks.tile([P, BLOCKS, P], F32, tag="in_bank")
            transpose_words(nc, h_bank, h_words[:, t * WORDS : (t + 1) * WORDS], ident)
            nc.scalar.copy(out=grouped_words[:, t, :, :, :], in_=words_by_column(h_bank))

        def transpose_in(i):
            for t in range(TILES):
                transpose_tile(i, t)

        def quantise(i):
            codes = mx_pool.tile([P, TILES * PASSES * P], U32, name="h_codes", align_bytes=64)
            scales = mx_pool.tile([P, TILES * PASSES * P], U8, name="h_scales", align_bytes=64)
            nc.vector.quantize_mx(out=codes[:].bitcast(FP8X4), scales=scales[:], in_=tiles["grouped", i][:])
            tiles["mx", i] = codes, scales

        w_grouped = consts.tile([P, PASSES * C * 4], BF16, align_bytes=64)
        w_grouped_words = w_grouped[:].bitcast(F32).rearrange(
            "p (g e q u) -> p g e q u", g=PASSES, e=PARITIES, u=2
        )
        for j in range(PARITIES):
            w_bank = in_banks.tile([P, BLOCKS, P], F32, tag="in_bank")
            transpose_words(nc, w_bank, w_sb[:, j, :].bitcast(F32), ident)
            nc.vector.tensor_copy(out=w_grouped_words[:, :, j, :, :], in_=words_by_column(w_bank))
            transpose_tile(0, j)
        w_codes = consts.tile([P, PASSES * C], U32, align_bytes=64)
        w_scales = consts.tile([P, PASSES * C], U8, align_bytes=64)
        nc.vector.quantize_mx(out=w_codes[:].bitcast(FP8X4), scales=w_scales[:], in_=w_grouped[:])
        quantise(0)

        row_bank = out_banks.tile([P, ROW], F32, tag="out_bank")
        nc.tensor.matmul(out=row_bank[:], lhsT=ones[:], rhs=row[:], start=True, stop=True)
        bias_bc = consts.tile([P, C], F32)
        nc.vector.tensor_copy(
            out=bias_bc[:].rearrange("p (e q) -> p e q", e=PARITIES),
            in_=row_bank[:, 0:C].rearrange("p (q e) -> p e q", e=PARITIES),
        )
        s_col = consts.tile([P, 1], F32)
        nc.vector.tensor_copy(out=s_col[:], in_=row_bank[:, S_AT : S_AT + 1])
        n_col = consts.tile([P, 1], F32)
        nc.vector.tensor_copy(out=n_col[:], in_=row_bank[:, N_AT : N_AT + 1])
        var_scale = consts.tile([P, 1], F32)
        nc.vector.tensor_scalar(
            out=var_scale[:], in0=s_col[:], scalar1=s_col[:, 0:1], scalar2=1.0 / C**3, op0=ALU.mult, op1=ALU.mult
        )
        gain = consts.tile([P, PARITIES], F32)
        nc.vector.tensor_scalar(
            out=gain[:], in0=ln_w[:], scalar1=n_col[:, 0:1], scalar2=s_col[:, 0:1], op0=ALU.mult, op1=ALU.mult
        )
        shift = consts.tile([P, PARITIES], F32)
        nc.vector.tensor_scalar(out=shift[:], in0=ln_b[:], scalar1=n_col[:, 0:1], scalar2=None, op0=ALU.mult)
        transpose_in(1)
        quantise(1)

        def multiply(i):
            codes, scales = tiles["mx", i]
            acc = acc_banks.tile([P, TILES, C], F32, name="acc")
            for t in range(TILES):
                for g in range(PASSES):
                    px = slice((t * PASSES + g) * P, (t * PASSES + g + 1) * P)
                    ch = slice(g * C, (g + 1) * C)
                    nc.tensor.matmul_mx(
                        out=acc[:, t, :],
                        lhsT=codes[:, px].bitcast(FP8X4),
                        lhsT_scale=scales[:, px],
                        rhs=w_codes[:, ch].bitcast(FP8X4),
                        rhs_scale=w_scales[:, ch],
                        start=(g == 0),
                        stop=(g == PASSES - 1),
                    )
            tiles["acc", i] = acc

        def add_bias(i):
            n, b = divmod(i, LOAD)
            if b == 0:
                tiles["v_sum", n] = stats.tile([P, LOAD, TILES], F32, name="v_sum")
            v = work.tile([P, TILES, C], F32, name="v")
            for t in range(TILES):
                nc.vector.scalar_tensor_tensor(
                    out=v[:, t, :],
                    in0=tiles["acc", i][:, t, :],
                    scalar=1.0,
                    in1=bias_bc[:],
                    op0=ALU.mult,
                    op1=ALU.add,
                    accum_out=tiles["v_sum", n][:, b, t : t + 1],
                )
            tiles["v", i] = v

        def squares(i):
            n, b = divmod(i, LOAD)
            squared = work.tile([P, TILES, C], F32, name="squared")
            sq_sum = stats.tile([P, TILES], F32, name="sq_sum")
            for t in range(TILES):
                nc.scalar.activation(
                    out=squared[:, t, :],
                    in_=tiles["v", i][:, t, :],
                    func=ACT.Square,
                    bias=tiles["v_sum", n][:, b, t : t + 1],
                    scale=-float(C),
                    accum_out=sq_sum[:, t : t + 1],
                )
            tiles["sq_sum", i] = sq_sum

        def mean(n):
            neg_mean = stats.tile([P, LOAD, TILES], F32, name="neg_mean")
            nc.vector.tensor_scalar(
                out=neg_mean[:], in0=tiles["v_sum", n][:], scalar1=-1.0 / C, scalar2=None, op0=ALU.mult
            )
            tiles["neg_mean", n] = neg_mean

        def inverse_std(i):
            rstd = stats.tile([P, TILES], F32, name="rstd")
            nc.scalar.activation(
                out=rstd[:],
                in_=tiles["sq_sum", i][:],
                func=ACT.Abs_reciprocal_sqrt,
                bias=eps_col[:, 0:1],
                scale=var_scale[:, 0:1],
            )
            tiles["rstd", i] = rstd
            tiles["normed", i] = work.tile([P, TILES, C], F32, name="normed")

        def normalise(engine, i, t):
            n, b = divmod(i, LOAD)
            engine.tensor_scalar(
                out=tiles["normed", i][:, t, :],
                in0=tiles["v", i][:, t, :],
                scalar1=tiles["neg_mean", n][:, b, t : t + 1],
                scalar2=tiles["rstd", i][:, t : t + 1],
                op0=ALU.add,
                op1=ALU.mult,
            )

        def transpose_out(n, e):
            o_bank = out_banks.tile([P, TILES, LOAD, P], F32, tag="out_bank")
            for b in range(LOAD):
                for t in range(TILES):
                    nc.tensor.transpose(
                        o_bank[:, t, b, :], tiles["normed", n * LOAD + b][:, t, e * P : (e + 1) * P], ident[:]
                    )
            tiles["o_bank", n, e] = o_bank

        def add_x(n, e):
            if e == 0:
                tiles["o", n] = work.tile([P, LOAD, PARITIES, IMAGE], F32, name="o_sb", bufs=4)
            nc.vector.scalar_tensor_tensor(
                out=tiles["o", n][:, :, e, :].rearrange("q b (p t) -> q b p t", t=TILES),
                in0=tiles["o_bank", n, e][:].rearrange("q t b p -> q b p t"),
                scalar=gain[:, e : e + 1],
                in1=tiles["x", n][:, :, e, :].rearrange("q b (p t) -> q b p t", t=TILES),
                op0=ALU.mult,
                op1=ALU.add,
            )

        def relu(n, e):
            half = tiles["o", n][:, :, e, :]
            if n % 4 == 2 and e == 0:
                nc.vector.tensor_scalar(
                    out=half, in0=half, scalar1=shift[:, e : e + 1], scalar2=0.0, op0=ALU.add, op1=ALU.max
                )
            else:
                nc.scalar.activation(out=half, in_=half, func=ACT.Relu, bias=shift[:, e : e + 1], scale=1.0)

        def store(n):
            nc.sync.dma_start(
                out=out[n * LOAD : (n + 1) * LOAD].rearrange("b (q e) i j -> q b (e i j)", e=PARITIES),
                in_=tiles["o", n][:].rearrange("q b e s -> q b (e s)"),
            )

        def is_image(i):
            return 0 <= i < IMAGES

        for step in range(IMAGES + 9):
            if step % LOAD == 0:
                if step // LOAD + PREFETCH < LOADS:
                    load_h(step // LOAD + PREFETCH)
                if step // LOAD + X_PREFETCH < LOADS:
                    load_x(step // LOAD + X_PREFETCH)
            if is_image(step - 1):
                squares(step - 1)
            if is_image(step + 2):
                transpose_in(step + 2)
            if is_image(step):
                multiply(step)
            if is_image(step - 3):
                normalise(nc.vector, step - 3, 0)
            if is_image(step - 5):
                transpose_out(*divmod(step - 5, LOAD))
            if is_image(step - 1):
                inverse_std(step - 1)
            if is_image(step):
                add_bias(step)
            if is_image(step - 5):
                add_x(*divmod(step - 5, LOAD))
            if is_image(step - 7):
                relu(*divmod(step - 7, LOAD))
            if is_image(step) and (step) % LOAD == LOAD - 1:
                mean((step) // LOAD)
            if is_image(step + 2):
                quantise(step + 2)
            if is_image(step - 3):
                normalise(nc.gpsimd, step - 3, 1)
            if is_image(step - 8) and (step - 8) % LOAD == LOAD - 1:
                store((step - 8) // LOAD)
